import numpy as np
import ml_dtypes


def mxq(x, axis, fmt="e4m3"):
    dtype, down = {"e4m3": (ml_dtypes.float8_e4m3fn, 7), "e5m2": (ml_dtypes.float8_e5m2, 14)}[fmt]
    v = np.moveaxis(np.asarray(x, np.float32).astype(ml_dtypes.bfloat16).astype(np.float64), axis, -1)
    blocks = v.reshape(v.shape[:-1] + (-1, 32))
    amax = np.abs(blocks).max(-1, keepdims=True)
    byte = np.maximum(np.where(amax > 0, np.frexp(amax)[1] - 1 + 127, 0) - down, 1)
    scale = np.exp2(byte - 127.0)
    codes = (blocks / scale).astype(np.float32).astype(dtype).astype(np.float64)
    return np.moveaxis((codes * scale).reshape(v.shape), -1, axis)


WIDE = False


def mx_kscale(k):
    if not WIDE:
        return np.ones(k)
    levels = np.array([10, -10, 5, -5, 0])
    a = np.random.permutation(np.resize(levels, k // 512 * 4)).reshape(k // 512, 4)
    idx = np.arange(k)
    return np.exp2(a[idx // 512, idx % 128 // 32])


BF16 = ml_dtypes.bfloat16


def bf(x):
    return np.asarray(x, np.float32).astype(BF16)


def f64(x):
    return np.asarray(x).astype(np.float64)


B, S, D, H, C = 1, 128, 512, 512, 512
F = 2 * D
LN_EPS = 1e-5


def erf(u):
    a = np.clip(u, -6.0, 6.0)
    w = 2.0 * a * a
    term = a.copy()
    tot = a.copy()
    for n in range(1, 100):
        term = term * w / (2 * n + 1)
        tot = tot + term
    return 2.0 / np.sqrt(np.pi) * np.exp(-a * a) * tot


def gelu_erf(z):
    return 0.5 * z * (1.0 + erf(z / np.sqrt(2.0)))


def setup_inputs():
    s = mx_kscale(H)
    return {"h_ret": bf(np.random.standard_normal((B, S, H)) * 3.0 * s),
            "x": bf(np.random.standard_normal((B, S, D))),
            "W1": bf(np.random.standard_normal((F, H)) * 0.3 / np.sqrt(H) / s),
            "b1": bf(np.random.standard_normal(F) * 0.2),
            "W2": bf(np.random.standard_normal((D, F)) * 1.5 / np.sqrt(F)),
            "b2": bf(np.random.standard_normal(D) * 0.2),
            "ln_g": bf(1.0 + 0.1 * np.random.standard_normal(D)),
            "ln_b": bf(0.1 * np.random.standard_normal(D))}


def reference(h_ret, x, W1, b1, W2, b2, ln_g, ln_b):
    z = (mxq(f64(h_ret), 2, "e4m3") @ mxq(f64(W1), 1, "e4m3").T) + f64(b1)
    g = gelu_erf(z)
    o = (mxq(g, 2, "e4m3") @ mxq(f64(W2), 1, "e4m3").T) + f64(b2)
    y = f64(x) + o
    mu = y.mean(-1, keepdims=True)
    var = np.square(y - mu).mean(-1, keepdims=True)
    return (y - mu) / np.sqrt(var + LN_EPS) * f64(ln_g) + f64(ln_b)

@@ -1,0 +1,216 @@
+from contextlib import ExitStack
+
+import concourse.mybir as mybir
+from concourse.masks import make_identity
+
+F32 = mybir.dt.float32
+BF16 = mybir.dt.bfloat16
+U32 = mybir.dt.uint32
+U8 = mybir.dt.uint8
+FP8X4 = mybir.dt.float8_e4m3fn_x4
+ACT = mybir.ActivationFunctionType
+ALU = mybir.AluOpType
+
+P = 128
+H = 512
+F = 1024
+D = 512
+LN_EPS = 1e-5
+PIECES = 4
+VECTOR_PIECES = 1
+
+FLOPS = 2 * P * H * F + 2 * P * F * D
+
+
+def tile_simplifiedretnet_pb_s_kernel(tc, h_ret, x, W1, b1, W2, b2, ln_g, ln_b, out):
+    nc = tc.nc
+    h_rows = h_ret.flatten_outer_dims()
+    x_rows = x.flatten_outer_dims()
+    out_rows = out.flatten_outer_dims()
+
+    with ExitStack() as stack:
+        keep = stack.enter_context(tc.tile_pool(name="keep", bufs=1))
+        stage = stack.enter_context(tc.tile_pool(name="stage", bufs=4))
+        psum_t = stack.enter_context(tc.psum_pool(name="psum_t", bufs=4))
+        psum_z = stack.enter_context(tc.psum_pool(name="psum_z", bufs=2))
+        psum_o = stack.enter_context(tc.psum_pool(name="psum_o", bufs=2))
+        stack.enter_context(tc.manual_schedule())
+
+        ident = keep.tile([P, P], F32)
+        vec_rows = keep.tile([P, 2 * P], BF16)
+        h_sb = keep.tile([P, H], BF16)
+        x_sb = keep.tile([P, D], BF16)
+        w1_sb = keep.tile([P, PIECES, 2 * H], BF16)
+        w2_sb = keep.tile([P, PIECES, F], BF16)
+        h_codes = keep.tile([P, P], U32, align_bytes=64)
+        h_scales = keep.tile([P, P], U8, align_bytes=64)
+        w1_codes = keep.tile([P, F], U32, align_bytes=64)
+        w1_scales = keep.tile([P, F], U8, align_bytes=64)
+        w2_codes = keep.tile([P, 2 * D], U32, align_bytes=64)
+        w2_scales = keep.tile([P, 2 * D], U8, align_bytes=64)
+        g_codes = keep.tile([P, 2 * P], U32, align_bytes=64)
+        g_scales = keep.tile([P, 2 * P], U8, align_bytes=64)
+        b1_cols = keep.tile([P, 8], F32)
+        vec_cols = keep.tile([P, 6], F32)
+        table_warm = keep.tile([P, 2], F32)
+        xb = keep.tile([P, D], F32)
+        y = keep.tile([P, D], F32)
+        centred = keep.tile([P, D], F32)
+        result = keep.tile([P, D], F32)
+        stats = keep.tile([P, 2, 6], F32)
+        mean_var = keep.tile([P, 2], F32)
+        std = keep.tile([P, 1], F32)
+        rstd = keep.tile([P, 1], F32)
+
+        def k_onto_partitions(words, copy):
+            chunks = words.shape[1] // P
+            bank = psum_t.tile([P, chunks, P], F32, tag="bank")
+            for n in range(chunks):
+                nc.tensor.transpose(bank[:, n, :], words[:, n * P : (n + 1) * P], ident[:])
+            grouped = stage.tile([P, chunks // 2, P, 2], F32, tag="grouped", align_bytes=64)
+            copy(out=grouped[:], in_=bank[:].rearrange("q (s u) r -> q s r u", u=2))
+            return grouped[:].rearrange("q s r u -> q (s r u)").bitcast(BF16)
+
+        def quantise(values, codes, scales):
+            nc.vector.quantize_mx(out=codes.bitcast(FP8X4), scales=scales, in_=values)
+
+        def bank_copy(piece):
+            return nc.vector.tensor_copy if piece < VECTOR_PIECES else nc.scalar.copy
+
+        def spread_over_partitions(bank, first, count):
+            for r in range(count):
+                nc.tensor.transpose(
+                    bank[:, r, :], vec_cols[:, first + r : first + r + 1].to_broadcast([P, P]), ident[:]
+                )
+
+        nc.vector.memset(vec_rows[:], 0.0)
+        nc.vector.memset(table_warm[:], 1.0)
+        nc.vector.memset(ident[:], 0.0)
+        make_identity(nc, ident[:], nomemset=True)
+        nc.scalar.dma_start(out=vec_rows[0:4, :], in_=b1.rearrange("(r c) -> r c", c=2 * P))
+        nc.scalar.dma_start(out=vec_rows[4:6, :], in_=b2.rearrange("(r c) -> r c", c=2 * P))
+        nc.scalar.dma_start(out=vec_rows[6:8, :], in_=ln_g.rearrange("(r c) -> r c", c=2 * P))
+        nc.scalar.dma_start(out=vec_rows[8:10, :], in_=ln_b.rearrange("(r c) -> r c", c=2 * P))
+        nc.sync.dma_start(out=h_sb[:], in_=h_rows)
+        for j in range(PIECES):
+            nc.sync.dma_start(
+                out=w1_sb[:, j, :],
+                in_=W1[2 * P * j : 2 * P * (j + 1), :].rearrange("(p e) k -> p (e k)", e=2),
+            )
+        nc.gpsimd.dma_start(out=x_sb[:], in_=x_rows)
+        for i in range(PIECES):
+            nc.sync.dma_start(out=w2_sb[:, i, :], in_=W2[P * i : P * (i + 1), :])
+        nc.scalar.activation(out=table_warm[:, 0:1], in_=table_warm[:, 0:1], func=ACT.Gelu)
+
+        cols_bank = psum_t.tile([P, P], F32, tag="bank")
+        nc.tensor.transpose(cols_bank[:], vec_rows[:].bitcast(F32), ident[:])
+        nc.vector.tensor_copy(out=b1_cols[:], in_=cols_bank[:, 0:4].bitcast(BF16))
+        nc.vector.tensor_copy(out=vec_cols[:], in_=cols_bank[:, 4:10])
+
+        h_grouped = k_onto_partitions(h_sb[:].bitcast(F32), nc.vector.tensor_copy)
+        b2_bank = psum_o.tile([P, 2, P], F32, tag="acc")
+        spread_over_partitions(b2_bank, 0, 2)
+        quantise(h_grouped, h_codes[:], h_scales[:])
+
+        for j in range(PIECES):
+            w1_grouped = k_onto_partitions(w1_sb[:, j, :].bitcast(F32), bank_copy(j))
+            cols = slice(2 * P * j, 2 * P * (j + 1))
+            quantise(w1_grouped, w1_codes[:, cols], w1_scales[:, cols])
+
+        nc.vector.tensor_tensor(
+            out=xb[:], in0=x_sb[:], in1=b2_bank[:].rearrange("i r q -> i (r q)").bitcast(BF16), op=ALU.add
+        )
+
+        def hidden_pass(c):
+            z_bank = psum_z.tile([P, 4, P], F32, tag="z")
+            g_plain = stage.tile([P, 4, P], BF16, tag="g_plain")
+            for t in range(4):
+                a = 4 * c + t
+                nc.tensor.matmul_mx(
+                    out=z_bank[:, t, :],
+                    lhsT=w1_codes[:, a * P : (a + 1) * P].bitcast(FP8X4),
+                    lhsT_scale=w1_scales[:, a * P : (a + 1) * P],
+                    rhs=h_codes[:].bitcast(FP8X4),
+                    rhs_scale=h_scales[:],
+                    start=True,
+                    stop=True,
+                )
+            for t in range(4):
+                a = 4 * c + t
+                nc.scalar.activation(
+                    out=g_plain[:, t, :], in_=z_bank[:, t, :], func=ACT.Gelu, bias=b1_cols[:, a : a + 1]
+                )
+            return g_plain
+
+        def regroup_g(g_plain):
+            g_grouped = stage.tile([P, P, 4], BF16, tag="g_grouped", align_bytes=64)
+            nc.vector.tensor_copy(out=g_grouped[:], in_=g_plain[:].rearrange("p t r -> p r t"))
+            return g_grouped[:].rearrange("p r t -> p (r t)")
+
+        def quantise_g(c, g_grouped):
+            quantise(g_grouped, g_codes[:, c * P : (c + 1) * P], g_scales[:, c * P : (c + 1) * P])
+
+        def quantise_w2(i, w2_grouped):
+            for c in range(2):
+                first = (i // 2) * D + c * 2 * P + (i % 2) * P
+                quantise(
+                    w2_grouped[:, c * H : (c + 1) * H],
+                    w2_codes[:, first : first + P],
+                    w2_scales[:, first : first + P],
+                )
+
+        g_plain = hidden_pass(0)
+        g_grouped = regroup_g(g_plain)
+        w2_grouped = [None] * PIECES
+        for i in (0, 1):
+            w2_grouped[i] = k_onto_partitions(w2_sb[:, i, :].bitcast(F32), bank_copy(i))
+        quantise_g(0, g_grouped)
+        for i in (0, 1):
+            quantise_w2(i, w2_grouped[i])
+
+        g_plain = hidden_pass(1)
+        for i in (2, 3):
+            w2_grouped[i] = k_onto_partitions(w2_sb[:, i, :].bitcast(F32), bank_copy(i))
+        nc.scalar.activation(out=table_warm[:, 1:2], in_=table_warm[:, 1:2], func=ACT.Sqrt)
+        quantise_w2(2, w2_grouped[2])
+        g_grouped = regroup_g(g_plain)
+        quantise_g(1, g_grouped)
+        quantise_w2(3, w2_grouped[3])
+
+        for half in range(2):
+            o_bank = psum_o.tile([P, D // 2], F32, tag="acc")
+            for c in range(2):
+                first = half * D + c * 2 * P
+                nc.tensor.matmul_mx(
+                    out=o_bank[:],
+                    lhsT=g_codes[:, c * P : (c + 1) * P].bitcast(FP8X4),
+                    lhsT_scale=g_scales[:, c * P : (c + 1) * P],
+                    rhs=w2_codes[:, first : first + 2 * P].bitcast(FP8X4),
+                    rhs_scale=w2_scales[:, first : first + 2 * P],
+                    start=(c == 0),
+                    stop=(c == 1),
+                )
+            cols = slice(half * (D // 2), (half + 1) * (D // 2))
+            nc.vector.tensor_tensor(out=y[:, cols], in0=o_bank[:], in1=xb[:, cols], op=ALU.add)
+            nc.vector.bn_stats(out=stats[:, half, :], in_=y[:, cols])
+        gb_bank = psum_t.tile([P, 4, P], F32, tag="bank")
+        spread_over_partitions(gb_bank, 2, 4)
+        gb = gb_bank[:].rearrange("i r q -> i (r q)").bitcast(BF16)
+
+        nc.vector.bn_aggr(out=mean_var[:], in_=stats[:].rearrange("p h s -> p (h s)"))
+        nc.scalar.activation(out=std[:], in_=mean_var[:, 1:2], func=ACT.Sqrt, bias=LN_EPS)
+        nc.vector.scalar_tensor_tensor(
+            out=centred[:], in0=y[:], scalar=mean_var[:, 0:1], in1=gb[:, 0:D], op0=ALU.subtract, op1=ALU.mult
+        )
+        nc.vector.reciprocal(out=rstd[:], in_=std[:])
+        for half, queue in enumerate((nc.sync, nc.scalar)):
+            cols = slice(half * (D // 2), (half + 1) * (D // 2))
+            nc.vector.scalar_tensor_tensor(
+                out=result[:, cols],
+                in0=centred[:, cols],
+                scalar=rstd[:, 0:1],
+                in1=gb[:, D + half * (D // 2) : D + (half + 1) * (D // 2)],
+                op0=ALU.mult,
+                op1=ALU.add,
+            )
+            queue.dma_start(out=out_rows[:, cols], in_=result[:, cols])

@@ -17,7 +17,6 @@ F = 1024
 D = 512
 LN_EPS = 1e-5
 PIECES = 4
-VECTOR_PIECES = 1
 
 FLOPS = 2 * P * H * F + 2 * P * F * D
 
@@ -34,7 +33,6 @@ def tile_simplifiedretnet_pb_s_kernel(tc, h_ret, x, W1, b1, W2, b2, ln_g, ln_b, 
         psum_t = stack.enter_context(tc.psum_pool(name="psum_t", bufs=4))
         psum_z = stack.enter_context(tc.psum_pool(name="psum_z", bufs=2))
         psum_o = stack.enter_context(tc.psum_pool(name="psum_o", bufs=2))
-        stack.enter_context(tc.manual_schedule())
 
         ident = keep.tile([P, P], F32)
         vec_rows = keep.tile([P, 2 * P], BF16)
@@ -75,7 +73,7 @@ def tile_simplifiedretnet_pb_s_kernel(tc, h_ret, x, W1, b1, W2, b2, ln_g, ln_b, 
             nc.vector.quantize_mx(out=codes.bitcast(FP8X4), scales=scales, in_=values)
 
         def bank_copy(piece):
-            return nc.vector.tensor_copy if piece < VECTOR_PIECES else nc.scalar.copy
+            return nc.vector.tensor_copy if piece % 2 == 0 else nc.scalar.copy
 
         def spread_over_partitions(bank, first, count):
             for r in range(count):
@@ -87,11 +85,11 @@ def tile_simplifiedretnet_pb_s_kernel(tc, h_ret, x, W1, b1, W2, b2, ln_g, ln_b, 
         nc.vector.memset(table_warm[:], 1.0)
         nc.vector.memset(ident[:], 0.0)
         make_identity(nc, ident[:], nomemset=True)
+        nc.sync.dma_start(out=h_sb[:], in_=h_rows)
         nc.scalar.dma_start(out=vec_rows[0:4, :], in_=b1.rearrange("(r c) -> r c", c=2 * P))
         nc.scalar.dma_start(out=vec_rows[4:6, :], in_=b2.rearrange("(r c) -> r c", c=2 * P))
         nc.scalar.dma_start(out=vec_rows[6:8, :], in_=ln_g.rearrange("(r c) -> r c", c=2 * P))
         nc.scalar.dma_start(out=vec_rows[8:10, :], in_=ln_b.rearrange("(r c) -> r c", c=2 * P))
-        nc.sync.dma_start(out=h_sb[:], in_=h_rows)
         for j in range(PIECES):
             nc.sync.dma_start(
                 out=w1_sb[:, j, :],
@@ -102,12 +100,12 @@ def tile_simplifiedretnet_pb_s_kernel(tc, h_ret, x, W1, b1, W2, b2, ln_g, ln_b, 
             nc.sync.dma_start(out=w2_sb[:, i, :], in_=W2[P * i : P * (i + 1), :])
         nc.scalar.activation(out=table_warm[:, 0:1], in_=table_warm[:, 0:1], func=ACT.Gelu)
 
+        h_grouped = k_onto_partitions(h_sb[:].bitcast(F32), nc.vector.tensor_copy)
+
         cols_bank = psum_t.tile([P, P], F32, tag="bank")
         nc.tensor.transpose(cols_bank[:], vec_rows[:].bitcast(F32), ident[:])
         nc.vector.tensor_copy(out=b1_cols[:], in_=cols_bank[:, 0:4].bitcast(BF16))
         nc.vector.tensor_copy(out=vec_cols[:], in_=cols_bank[:, 4:10])
-
-        h_grouped = k_onto_partitions(h_sb[:].bitcast(F32), nc.vector.tensor_copy)
         b2_bank = psum_o.tile([P, 2, P], F32, tag="acc")
         spread_over_partitions(b2_bank, 0, 2)
         quantise(h_grouped, h_codes[:], h_scales[:])
@@ -171,10 +169,9 @@ def tile_simplifiedretnet_pb_s_kernel(tc, h_ret, x, W1, b1, W2, b2, ln_g, ln_b, 
         g_plain = hidden_pass(1)
         for i in (2, 3):
             w2_grouped[i] = k_onto_partitions(w2_sb[:, i, :].bitcast(F32), bank_copy(i))
-        nc.scalar.activation(out=table_warm[:, 1:2], in_=table_warm[:, 1:2], func=ACT.Sqrt)
-        quantise_w2(2, w2_grouped[2])
         g_grouped = regroup_g(g_plain)
         quantise_g(1, g_grouped)
+        quantise_w2(2, w2_grouped[2])
         quantise_w2(3, w2_grouped[3])
 
         for half in range(2):

@@ -18,6 +18,8 @@ D = 512
 LN_EPS = 1e-5
 PIECES = 4
 
+WARM_PASSES = 16
+
 FLOPS = 2 * P * H * F + 2 * P * F * D
 
 
@@ -51,6 +53,9 @@ def tile_simplifiedretnet_pb_s_kernel(tc, h_ret, x, W1, b1, W2, b2, ln_g, ln_b, 
         b1_cols = keep.tile([P, 8], F32)
         vec_cols = keep.tile([P, 6], F32)
         table_warm = keep.tile([P, 2], F32)
+        zero_values = keep.tile([P, 4 * P], BF16, align_bytes=64)
+        zero_codes = keep.tile([P, P], U32, align_bytes=64)
+        zero_scales = keep.tile([P, P], U8, align_bytes=64)
         xb = keep.tile([P, D], F32)
         y = keep.tile([P, D], F32)
         centred = keep.tile([P, D], F32)
@@ -81,6 +86,7 @@ def tile_simplifiedretnet_pb_s_kernel(tc, h_ret, x, W1, b1, W2, b2, ln_g, ln_b, 
                     bank[:, r, :], vec_cols[:, first + r : first + r + 1].to_broadcast([P, P]), ident[:]
                 )
 
+        nc.vector.memset(zero_values[:], 0.0)
         nc.vector.memset(vec_rows[:], 0.0)
         nc.vector.memset(table_warm[:], 1.0)
         nc.vector.memset(ident[:], 0.0)
@@ -99,6 +105,19 @@ def tile_simplifiedretnet_pb_s_kernel(tc, h_ret, x, W1, b1, W2, b2, ln_g, ln_b, 
         for i in range(PIECES):
             nc.sync.dma_start(out=w2_sb[:, i, :], in_=W2[P * i : P * (i + 1), :])
         nc.scalar.activation(out=table_warm[:, 0:1], in_=table_warm[:, 0:1], func=ACT.Gelu)
+
+        quantise(zero_values[:], zero_codes[:], zero_scales[:])
+        idle_bank = psum_z.tile([P, P], F32, tag="z")
+        for n in range(WARM_PASSES):
+            nc.tensor.matmul_mx(
+                out=idle_bank[:],
+                lhsT=zero_codes[:].bitcast(FP8X4),
+                lhsT_scale=zero_scales[:],
+                rhs=zero_codes[:].bitcast(FP8X4),
+                rhs_scale=zero_scales[:],
+                start=True,
+                stop=True,
+            )
 
         h_grouped = k_onto_partitions(h_sb[:].bitcast(F32), nc.vector.tensor_copy)
 

@@ -18,8 +18,6 @@ D = 512
 LN_EPS = 1e-5
 PIECES = 4
 
-WARM_PASSES = 16
-
 FLOPS = 2 * P * H * F + 2 * P * F * D
 
 
@@ -37,7 +35,8 @@ def tile_simplifiedretnet_pb_s_kernel(tc, h_ret, x, W1, b1, W2, b2, ln_g, ln_b, 
         psum_o = stack.enter_context(tc.psum_pool(name="psum_o", bufs=2))
 
         ident = keep.tile([P, P], F32)
-        vec_rows = keep.tile([P, 2 * P], BF16)
+        bias_rows = keep.tile([P, 2 * P], BF16)
+        norm_rows = keep.tile([P, 2 * P], BF16)
         h_sb = keep.tile([P, H], BF16)
         x_sb = keep.tile([P, D], BF16)
         w1_sb = keep.tile([P, PIECES, 2 * H], BF16)
@@ -51,11 +50,9 @@ def tile_simplifiedretnet_pb_s_kernel(tc, h_ret, x, W1, b1, W2, b2, ln_g, ln_b, 
         g_codes = keep.tile([P, 2 * P], U32, align_bytes=64)
         g_scales = keep.tile([P, 2 * P], U8, align_bytes=64)
         b1_cols = keep.tile([P, 8], F32)
-        vec_cols = keep.tile([P, 6], F32)
+        b2_cols = keep.tile([P, 2], F32)
+        norm_cols = keep.tile([P, 4], F32)
         table_warm = keep.tile([P, 2], F32)
-        zero_values = keep.tile([P, 4 * P], BF16, align_bytes=64)
-        zero_codes = keep.tile([P, P], U32, align_bytes=64)
-        zero_scales = keep.tile([P, P], U8, align_bytes=64)
         xb = keep.tile([P, D], F32)
         y = keep.tile([P, D], F32)
         centred = keep.tile([P, D], F32)
@@ -80,59 +77,45 @@ def tile_simplifiedretnet_pb_s_kernel(tc, h_ret, x, W1, b1, W2, b2, ln_g, ln_b, 
         def bank_copy(piece):
             return nc.vector.tensor_copy if piece % 2 == 0 else nc.scalar.copy
 
-        def spread_over_partitions(bank, first, count):
-            for r in range(count):
-                nc.tensor.transpose(
-                    bank[:, r, :], vec_cols[:, first + r : first + r + 1].to_broadcast([P, P]), ident[:]
-                )
+        def spread_over_partitions(bank, cols):
+            for r in range(cols.shape[1]):
+                nc.tensor.transpose(bank[:, r, :], cols[:, r : r + 1].to_broadcast([P, P]), ident[:])
 
-        nc.vector.memset(zero_values[:], 0.0)
-        nc.vector.memset(vec_rows[:], 0.0)
+        nc.vector.memset(bias_rows[:], 0.0)
+        nc.vector.memset(norm_rows[:], 0.0)
         nc.vector.memset(table_warm[:], 1.0)
         nc.vector.memset(ident[:], 0.0)
         make_identity(nc, ident[:], nomemset=True)
         nc.sync.dma_start(out=h_sb[:], in_=h_rows)
-        nc.scalar.dma_start(out=vec_rows[0:4, :], in_=b1.rearrange("(r c) -> r c", c=2 * P))
-        nc.scalar.dma_start(out=vec_rows[4:6, :], in_=b2.rearrange("(r c) -> r c", c=2 * P))
-        nc.scalar.dma_start(out=vec_rows[6:8, :], in_=ln_g.rearrange("(r c) -> r c", c=2 * P))
-        nc.scalar.dma_start(out=vec_rows[8:10, :], in_=ln_b.rearrange("(r c) -> r c", c=2 * P))
         for j in range(PIECES):
             nc.sync.dma_start(
                 out=w1_sb[:, j, :],
                 in_=W1[2 * P * j : 2 * P * (j + 1), :].rearrange("(p e) k -> p (e k)", e=2),
             )
+        nc.sync.dma_start(out=bias_rows[0:4, :], in_=b1.rearrange("(r c) -> r c", c=2 * P))
+        nc.sync.dma_start(out=bias_rows[4:6, :], in_=b2.rearrange("(r c) -> r c", c=2 * P))
         nc.gpsimd.dma_start(out=x_sb[:], in_=x_rows)
         for i in range(PIECES):
             nc.sync.dma_start(out=w2_sb[:, i, :], in_=W2[P * i : P * (i + 1), :])
+        nc.sync.dma_start(out=norm_rows[0:2, :], in_=ln_g.rearrange("(r c) -> r c", c=2 * P))
+        nc.sync.dma_start(out=norm_rows[2:4, :], in_=ln_b.rearrange("(r c) -> r c", c=2 * P))
         nc.scalar.activation(out=table_warm[:, 0:1], in_=table_warm[:, 0:1], func=ACT.Gelu)
-
-        quantise(zero_values[:], zero_codes[:], zero_scales[:])
-        idle_bank = psum_z.tile([P, P], F32, tag="z")
-        for n in range(WARM_PASSES):
-            nc.tensor.matmul_mx(
-                out=idle_bank[:],
-                lhsT=zero_codes[:].bitcast(FP8X4),
-                lhsT_scale=zero_scales[:],
-                rhs=zero_codes[:].bitcast(FP8X4),
-                rhs_scale=zero_scales[:],
-                start=True,
-                stop=True,
-            )
 
         h_grouped = k_onto_partitions(h_sb[:].bitcast(F32), nc.vector.tensor_copy)
 
-        cols_bank = psum_t.tile([P, P], F32, tag="bank")
-        nc.tensor.transpose(cols_bank[:], vec_rows[:].bitcast(F32), ident[:])
-        nc.vector.tensor_copy(out=b1_cols[:], in_=cols_bank[:, 0:4].bitcast(BF16))
-        nc.vector.tensor_copy(out=vec_cols[:], in_=cols_bank[:, 4:10])
-        b2_bank = psum_o.tile([P, 2, P], F32, tag="acc")
-        spread_over_partitions(b2_bank, 0, 2)
         quantise(h_grouped, h_codes[:], h_scales[:])
 
         for j in range(PIECES):
             w1_grouped = k_onto_partitions(w1_sb[:, j, :].bitcast(F32), bank_copy(j))
             cols = slice(2 * P * j, 2 * P * (j + 1))
             quantise(w1_grouped, w1_codes[:, cols], w1_scales[:, cols])
+
+        bias_bank = psum_t.tile([P, P], F32, tag="bank")
+        nc.tensor.transpose(bias_bank[:], bias_rows[:].bitcast(F32), ident[:])
+        nc.vector.tensor_copy(out=b1_cols[:], in_=bias_bank[:, 0:4].bitcast(BF16))
+        nc.vector.tensor_copy(out=b2_cols[:], in_=bias_bank[:, 4:6])
+        b2_bank = psum_o.tile([P, 2, P], F32, tag="acc")
+        spread_over_partitions(b2_bank, b2_cols)
 
         nc.vector.tensor_tensor(
             out=xb[:], in0=x_sb[:], in1=b2_bank[:].rearrange("i r q -> i (r q)").bitcast(BF16), op=ALU.add
@@ -209,8 +192,11 @@ def tile_simplifiedretnet_pb_s_kernel(tc, h_ret, x, W1, b1, W2, b2, ln_g, ln_b, 
             cols = slice(half * (D // 2), (half + 1) * (D // 2))
             nc.vector.tensor_tensor(out=y[:, cols], in0=o_bank[:], in1=xb[:, cols], op=ALU.add)
             nc.vector.bn_stats(out=stats[:, half, :], in_=y[:, cols])
+        norm_bank = psum_t.tile([P, P], F32, tag="bank")
+        nc.tensor.transpose(norm_bank[:], norm_rows[:].bitcast(F32), ident[:])
+        nc.vector.tensor_copy(out=norm_cols[:], in_=norm_bank[:, 0:4])
         gb_bank = psum_t.tile([P, 4, P], F32, tag="bank")
-        spread_over_partitions(gb_bank, 2, 4)
+        spread_over_partitions(gb_bank, norm_cols)
         gb = gb_bank[:].rearrange("i r q -> i (r q)").bitcast(BF16)
 
         nc.vector.bn_aggr(out=mean_var[:], in_=stats[:].rearrange("p h s -> p (h s)"))
@@ -219,7 +205,7 @@ def tile_simplifiedretnet_pb_s_kernel(tc, h_ret, x, W1, b1, W2, b2, ln_g, ln_b, 
             out=centred[:], in0=y[:], scalar=mean_var[:, 0:1], in1=gb[:, 0:D], op0=ALU.subtract, op1=ALU.mult
         )
         nc.vector.reciprocal(out=rstd[:], in_=std[:])
-        for half, queue in enumerate((nc.sync, nc.scalar)):
+        for half in range(2):
             cols = slice(half * (D // 2), (half + 1) * (D // 2))
             nc.vector.scalar_tensor_tensor(
                 out=result[:, cols],
@@ -229,4 +215,4 @@ def tile_simplifiedretnet_pb_s_kernel(tc, h_ret, x, W1, b1, W2, b2, ln_g, ln_b, 
                 op0=ALU.mult,
                 op1=ALU.add,
             )
-            queue.dma_start(out=out_rows[:, cols], in_=result[:, cols])
+            nc.sync.dma_start(out=out_rows[:, cols], in_=result[:, cols])

@@ -30,9 +30,7 @@ def tile_simplifiedretnet_pb_s_kernel(tc, h_ret, x, W1, b1, W2, b2, ln_g, ln_b, 
     with ExitStack() as stack:
         keep = stack.enter_context(tc.tile_pool(name="keep", bufs=1))
         stage = stack.enter_context(tc.tile_pool(name="stage", bufs=4))
-        psum_t = stack.enter_context(tc.psum_pool(name="psum_t", bufs=4))
-        psum_z = stack.enter_context(tc.psum_pool(name="psum_z", bufs=2))
-        psum_o = stack.enter_context(tc.psum_pool(name="psum_o", bufs=2))
+        psum = stack.enter_context(tc.psum_pool(name="psum", bufs=8))
 
         ident = keep.tile([P, P], F32)
         bias_rows = keep.tile([P, 2 * P], BF16)
@@ -62,20 +60,17 @@ def tile_simplifiedretnet_pb_s_kernel(tc, h_ret, x, W1, b1, W2, b2, ln_g, ln_b, 
         std = keep.tile([P, 1], F32)
         rstd = keep.tile([P, 1], F32)
 
-        def k_onto_partitions(words, copy):
-            chunks = words.shape[1] // P
-            bank = psum_t.tile([P, chunks, P], F32, tag="bank")
-            for n in range(chunks):
-                nc.tensor.transpose(bank[:, n, :], words[:, n * P : (n + 1) * P], ident[:])
-            grouped = stage.tile([P, chunks // 2, P, 2], F32, tag="grouped", align_bytes=64)
-            copy(out=grouped[:], in_=bank[:].rearrange("q (s u) r -> q s r u", u=2))
-            return grouped[:].rearrange("q s r u -> q (s r u)").bitcast(BF16)
-
         def quantise(values, codes, scales):
             nc.vector.quantize_mx(out=codes.bitcast(FP8X4), scales=scales, in_=values)
 
-        def bank_copy(piece):
-            return nc.vector.tensor_copy if piece % 2 == 0 else nc.scalar.copy
+        def quantise_rows(rows, codes, scales):
+            words = rows.bitcast(F32)
+            bank = psum.tile([P, 2, P], F32, tag="bank")
+            for u in range(2):
+                nc.tensor.transpose(bank[:, u, :], words[:, u * P : (u + 1) * P], ident[:])
+            grouped = stage.tile([P, P, 2], F32, tag="grouped", align_bytes=64)
+            nc.scalar.copy(out=grouped[:], in_=bank[:].rearrange("q u r -> q r u"))
+            quantise(grouped[:].rearrange("q r u -> q (r u)").bitcast(BF16), codes, scales)
 
         def spread_over_partitions(bank, cols):
             for r in range(cols.shape[1]):
@@ -101,20 +96,18 @@ def tile_simplifiedretnet_pb_s_kernel(tc, h_ret, x, W1, b1, W2, b2, ln_g, ln_b, 
         nc.sync.dma_start(out=norm_rows[2:4, :], in_=ln_b.rearrange("(r c) -> r c", c=2 * P))
         nc.scalar.activation(out=table_warm[:, 0:1], in_=table_warm[:, 0:1], func=ACT.Gelu)
 
-        h_grouped = k_onto_partitions(h_sb[:].bitcast(F32), nc.vector.tensor_copy)
+        quantise_rows(h_sb[:], h_codes[:], h_scales[:])
 
-        quantise(h_grouped, h_codes[:], h_scales[:])
 
-        for j in range(PIECES):
-            w1_grouped = k_onto_partitions(w1_sb[:, j, :].bitcast(F32), bank_copy(j))
-            cols = slice(2 * P * j, 2 * P * (j + 1))
-            quantise(w1_grouped, w1_codes[:, cols], w1_scales[:, cols])
+        for a in range(F // P):
+            cols = slice(a * P, (a + 1) * P)
+            quantise_rows(w1_sb[:, a // 2, (a % 2) * H : (a % 2 + 1) * H], w1_codes[:, cols], w1_scales[:, cols])
 
-        bias_bank = psum_t.tile([P, P], F32, tag="bank")
+        bias_bank = psum.tile([P, P], F32, tag="bank")
         nc.tensor.transpose(bias_bank[:], bias_rows[:].bitcast(F32), ident[:])
         nc.vector.tensor_copy(out=b1_cols[:], in_=bias_bank[:, 0:4].bitcast(BF16))
         nc.vector.tensor_copy(out=b2_cols[:], in_=bias_bank[:, 4:6])
-        b2_bank = psum_o.tile([P, 2, P], F32, tag="acc")
+        b2_bank = psum.tile([P, 2, P], F32, tag="bank")
         spread_over_partitions(b2_bank, b2_cols)
 
         nc.vector.tensor_tensor(
@@ -122,7 +115,7 @@ def tile_simplifiedretnet_pb_s_kernel(tc, h_ret, x, W1, b1, W2, b2, ln_g, ln_b, 
         )
 
         def hidden_pass(c):
-            z_bank = psum_z.tile([P, 4, P], F32, tag="z")
+            z_bank = psum.tile([P, 4, P], F32, tag="bank")
             g_plain = stage.tile([P, 4, P], BF16, tag="g_plain")
             for t in range(4):
                 a = 4 * c + t
@@ -150,34 +143,27 @@ def tile_simplifiedretnet_pb_s_kernel(tc, h_ret, x, W1, b1, W2, b2, ln_g, ln_b, 
         def quantise_g(c, g_grouped):
             quantise(g_grouped, g_codes[:, c * P : (c + 1) * P], g_scales[:, c * P : (c + 1) * P])
 
-        def quantise_w2(i, w2_grouped):
+        def quantise_w2(i):
             for c in range(2):
                 first = (i // 2) * D + c * 2 * P + (i % 2) * P
-                quantise(
-                    w2_grouped[:, c * H : (c + 1) * H],
-                    w2_codes[:, first : first + P],
-                    w2_scales[:, first : first + P],
+                quantise_rows(
+                    w2_sb[:, i, c * H : (c + 1) * H], w2_codes[:, first : first + P], w2_scales[:, first : first + P]
                 )
 
         g_plain = hidden_pass(0)
         g_grouped = regroup_g(g_plain)
-        w2_grouped = [None] * PIECES
-        for i in (0, 1):
-            w2_grouped[i] = k_onto_partitions(w2_sb[:, i, :].bitcast(F32), bank_copy(i))
         quantise_g(0, g_grouped)
         for i in (0, 1):
-            quantise_w2(i, w2_grouped[i])
+            quantise_w2(i)
 
         g_plain = hidden_pass(1)
-        for i in (2, 3):
-            w2_grouped[i] = k_onto_partitions(w2_sb[:, i, :].bitcast(F32), bank_copy(i))
         g_grouped = regroup_g(g_plain)
         quantise_g(1, g_grouped)
-        quantise_w2(2, w2_grouped[2])
-        quantise_w2(3, w2_grouped[3])
+        for i in (2, 3):
+            quantise_w2(i)
 
         for half in range(2):
-            o_bank = psum_o.tile([P, D // 2], F32, tag="acc")
+            o_bank = psum.tile([P, D // 2], F32, tag="bank")
             for c in range(2):
                 first = half * D + c * 2 * P
                 nc.tensor.matmul_mx(
@@ -192,10 +178,10 @@ def tile_simplifiedretnet_pb_s_kernel(tc, h_ret, x, W1, b1, W2, b2, ln_g, ln_b, 
             cols = slice(half * (D // 2), (half + 1) * (D // 2))
             nc.vector.tensor_tensor(out=y[:, cols], in0=o_bank[:], in1=xb[:, cols], op=ALU.add)
             nc.vector.bn_stats(out=stats[:, half, :], in_=y[:, cols])
-        norm_bank = psum_t.tile([P, P], F32, tag="bank")
+        norm_bank = psum.tile([P, P], F32, tag="bank")
         nc.tensor.transpose(norm_bank[:], norm_rows[:].bitcast(F32), ident[:])
         nc.vector.tensor_copy(out=norm_cols[:], in_=norm_bank[:, 0:4])
-        gb_bank = psum_t.tile([P, 4, P], F32, tag="bank")
+        gb_bank = psum.tile([P, 4, P], F32, tag="bank")
         spread_over_partitions(gb_bank, norm_cols)
         gb = gb_bank[:].rearrange("i r q -> i (r q)").bitcast(BF16)
 

@@ -30,7 +30,9 @@ def tile_simplifiedretnet_pb_s_kernel(tc, h_ret, x, W1, b1, W2, b2, ln_g, ln_b, 
     with ExitStack() as stack:
         keep = stack.enter_context(tc.tile_pool(name="keep", bufs=1))
         stage = stack.enter_context(tc.tile_pool(name="stage", bufs=4))
-        psum = stack.enter_context(tc.psum_pool(name="psum", bufs=8))
+        psum_t = stack.enter_context(tc.psum_pool(name="psum_t", bufs=4))
+        psum_z = stack.enter_context(tc.psum_pool(name="psum_z", bufs=2))
+        psum_o = stack.enter_context(tc.psum_pool(name="psum_o", bufs=2))
 
         ident = keep.tile([P, P], F32)
         bias_rows = keep.tile([P, 2 * P], BF16)
@@ -65,7 +67,7 @@ def tile_simplifiedretnet_pb_s_kernel(tc, h_ret, x, W1, b1, W2, b2, ln_g, ln_b, 
 
         def quantise_rows(rows, codes, scales):
             words = rows.bitcast(F32)
-            bank = psum.tile([P, 2, P], F32, tag="bank")
+            bank = psum_t.tile([P, 2, P], F32, tag="bank")
             for u in range(2):
                 nc.tensor.transpose(bank[:, u, :], words[:, u * P : (u + 1) * P], ident[:])
             grouped = stage.tile([P, P, 2], F32, tag="grouped", align_bytes=64)
@@ -103,11 +105,11 @@ def tile_simplifiedretnet_pb_s_kernel(tc, h_ret, x, W1, b1, W2, b2, ln_g, ln_b, 
             cols = slice(a * P, (a + 1) * P)
             quantise_rows(w1_sb[:, a // 2, (a % 2) * H : (a % 2 + 1) * H], w1_codes[:, cols], w1_scales[:, cols])
 
-        bias_bank = psum.tile([P, P], F32, tag="bank")
+        bias_bank = psum_t.tile([P, P], F32, tag="bank")
         nc.tensor.transpose(bias_bank[:], bias_rows[:].bitcast(F32), ident[:])
         nc.vector.tensor_copy(out=b1_cols[:], in_=bias_bank[:, 0:4].bitcast(BF16))
         nc.vector.tensor_copy(out=b2_cols[:], in_=bias_bank[:, 4:6])
-        b2_bank = psum.tile([P, 2, P], F32, tag="bank")
+        b2_bank = psum_o.tile([P, 2, P], F32, tag="acc")
         spread_over_partitions(b2_bank, b2_cols)
 
         nc.vector.tensor_tensor(
@@ -115,7 +117,7 @@ def tile_simplifiedretnet_pb_s_kernel(tc, h_ret, x, W1, b1, W2, b2, ln_g, ln_b, 
         )
 
         def hidden_pass(c):
-            z_bank = psum.tile([P, 4, P], F32, tag="bank")
+            z_bank = psum_z.tile([P, 4, P], F32, tag="z")
             g_plain = stage.tile([P, 4, P], BF16, tag="g_plain")
             for t in range(4):
                 a = 4 * c + t
@@ -163,7 +165,7 @@ def tile_simplifiedretnet_pb_s_kernel(tc, h_ret, x, W1, b1, W2, b2, ln_g, ln_b, 
             quantise_w2(i)
 
         for half in range(2):
-            o_bank = psum.tile([P, D // 2], F32, tag="bank")
+            o_bank = psum_o.tile([P, D // 2], F32, tag="acc")
             for c in range(2):
                 first = half * D + c * 2 * P
                 nc.tensor.matmul_mx(
@@ -178,10 +180,10 @@ def tile_simplifiedretnet_pb_s_kernel(tc, h_ret, x, W1, b1, W2, b2, ln_g, ln_b, 
             cols = slice(half * (D // 2), (half + 1) * (D // 2))
             nc.vector.tensor_tensor(out=y[:, cols], in0=o_bank[:], in1=xb[:, cols], op=ALU.add)
             nc.vector.bn_stats(out=stats[:, half, :], in_=y[:, cols])
-        norm_bank = psum.tile([P, P], F32, tag="bank")
+        norm_bank = psum_t.tile([P, P], F32, tag="bank")
         nc.tensor.transpose(norm_bank[:], norm_rows[:].bitcast(F32), ident[:])
         nc.vector.tensor_copy(out=norm_cols[:], in_=norm_bank[:, 0:4])
-        gb_bank = psum.tile([P, 4, P], F32, tag="bank")
+        gb_bank = psum_t.tile([P, 4, P], F32, tag="bank")
         spread_over_partitions(gb_bank, norm_cols)
         gb = gb_bank[:].rearrange("i r q -> i (r q)").bitcast(BF16)
 

@@ -57,9 +57,10 @@ def tile_simplifiedretnet_pb_s_kernel(tc, h_ret, x, W1, b1, W2, b2, ln_g, ln_b, 
         y = keep.tile([P, D], F32)
         centred = keep.tile([P, D], F32)
         result = keep.tile([P, D], F32)
-        stats = keep.tile([P, 2, 6], F32)
-        mean_var = keep.tile([P, 2], F32)
-        std = keep.tile([P, 1], F32)
+        squares = keep.tile([P, D], F32)
+        sums = keep.tile([P, 2], F32)
+        minus_mean = keep.tile([P, 1], F32)
+        square_sum = keep.tile([P, 1], F32)
         rstd = keep.tile([P, 1], F32)
 
         def quantise(values, codes, scales):
@@ -73,6 +74,7 @@ def tile_simplifiedretnet_pb_s_kernel(tc, h_ret, x, W1, b1, W2, b2, ln_g, ln_b, 
             grouped = stage.tile([P, P, 2], F32, tag="grouped", align_bytes=64)
             nc.scalar.copy(out=grouped[:], in_=bank[:].rearrange("q u r -> q r u"))
             quantise(grouped[:].rearrange("q r u -> q (r u)").bitcast(BF16), codes, scales)
+            return grouped
 
         def spread_over_partitions(bank, cols):
             for r in range(cols.shape[1]):
@@ -148,9 +150,10 @@ def tile_simplifiedretnet_pb_s_kernel(tc, h_ret, x, W1, b1, W2, b2, ln_g, ln_b, 
         def quantise_w2(i):
             for c in range(2):
                 first = (i // 2) * D + c * 2 * P + (i % 2) * P
-                quantise_rows(
+                grouped = quantise_rows(
                     w2_sb[:, i, c * H : (c + 1) * H], w2_codes[:, first : first + P], w2_scales[:, first : first + P]
                 )
+            return grouped
 
         g_plain = hidden_pass(0)
         g_grouped = regroup_g(g_plain)
@@ -162,7 +165,14 @@ def tile_simplifiedretnet_pb_s_kernel(tc, h_ret, x, W1, b1, W2, b2, ln_g, ln_b, 
         g_grouped = regroup_g(g_plain)
         quantise_g(1, g_grouped)
         for i in (2, 3):
-            quantise_w2(i)
+            grouped = quantise_w2(i)
+        nc.scalar.activation(
+            out=table_warm[:, 1:2],
+            in_=grouped[:, P - 1, :].bitcast(BF16)[:, 3:4],
+            func=ACT.Abs_reciprocal_sqrt,
+            scale=0.0,
+            bias=1.0,
+        )
 
         for half in range(2):
             o_bank = psum_o.tile([P, D // 2], F32, tag="acc")
@@ -178,8 +188,15 @@ def tile_simplifiedretnet_pb_s_kernel(tc, h_ret, x, W1, b1, W2, b2, ln_g, ln_b, 
                     stop=(c == 1),
                 )
             cols = slice(half * (D // 2), (half + 1) * (D // 2))
-            nc.vector.tensor_tensor(out=y[:, cols], in0=o_bank[:], in1=xb[:, cols], op=ALU.add)
-            nc.vector.bn_stats(out=stats[:, half, :], in_=y[:, cols])
+            nc.vector.scalar_tensor_tensor(
+                out=y[:, cols],
+                in0=o_bank[:],
+                scalar=1.0,
+                in1=xb[:, cols],
+                op0=ALU.mult,
+                op1=ALU.add,
+                accum_out=sums[:, half : half + 1],
+            )
         norm_bank = psum_t.tile([P, P], F32, tag="bank")
         nc.tensor.transpose(norm_bank[:], norm_rows[:].bitcast(F32), ident[:])
         nc.vector.tensor_copy(out=norm_cols[:], in_=norm_bank[:, 0:4])
@@ -187,12 +204,18 @@ def tile_simplifiedretnet_pb_s_kernel(tc, h_ret, x, W1, b1, W2, b2, ln_g, ln_b, 
         spread_over_partitions(gb_bank, norm_cols)
         gb = gb_bank[:].rearrange("i r q -> i (r q)").bitcast(BF16)
 
-        nc.vector.bn_aggr(out=mean_var[:], in_=stats[:].rearrange("p h s -> p (h s)"))
-        nc.scalar.activation(out=std[:], in_=mean_var[:, 1:2], func=ACT.Sqrt, bias=LN_EPS)
-        nc.vector.scalar_tensor_tensor(
-            out=centred[:], in0=y[:], scalar=mean_var[:, 0:1], in1=gb[:, 0:D], op0=ALU.subtract, op1=ALU.mult
+        nc.vector.tensor_scalar(
+            out=minus_mean[:], in0=sums[:, 0:1], scalar1=sums[:, 1:2], scalar2=-1.0 / D, op0=ALU.add, op1=ALU.mult
         )
-        nc.vector.reciprocal(out=rstd[:], in_=std[:])
+        nc.scalar.activation(
+            out=squares[:], in_=y[:], func=ACT.Square, bias=minus_mean[:, 0:1], accum_out=square_sum[:]
+        )
+        nc.vector.scalar_tensor_tensor(
+            out=centred[:], in0=y[:], scalar=minus_mean[:, 0:1], in1=gb[:, 0:D], op0=ALU.add, op1=ALU.mult
+        )
+        nc.scalar.activation(
+            out=rstd[:], in_=square_sum[:], func=ACT.Abs_reciprocal_sqrt, bias=LN_EPS, scale=1.0 / D
+        )
         for half in range(2):
             cols = slice(half * (D // 2), (half + 1) * (D // 2))
             nc.vector.scalar_tensor_tensor(

@@ -53,6 +53,7 @@ def tile_simplifiedretnet_pb_s_kernel(tc, h_ret, x, W1, b1, W2, b2, ln_g, ln_b, 
         b2_cols = keep.tile([P, 2], F32)
         norm_cols = keep.tile([P, 4], F32)
         table_warm = keep.tile([P, 2], F32)
+        zeros = keep.tile([P, 2 * P], F32)
         xb = keep.tile([P, D], F32)
         y = keep.tile([P, D], F32)
         centred = keep.tile([P, D], F32)
@@ -80,6 +81,10 @@ def tile_simplifiedretnet_pb_s_kernel(tc, h_ret, x, W1, b1, W2, b2, ln_g, ln_b, 
             for r in range(cols.shape[1]):
                 nc.tensor.transpose(bank[:, r, :], cols[:, r : r + 1].to_broadcast([P, P]), ident[:])
 
+        nc.gpsimd.memset(zeros[:], 0.0)
+        for bank in range(2):
+            idle_bank = psum_z.tile([P, 2 * P], F32, tag="z")
+            nc.tensor.matmul(idle_bank[:], lhsT=zeros[:, 0:P], rhs=zeros[:], start=True, stop=True)
         nc.vector.memset(bias_rows[:], 0.0)
         nc.vector.memset(norm_rows[:], 0.0)
         nc.vector.memset(table_warm[:], 1.0)
@@ -93,9 +98,9 @@ def tile_simplifiedretnet_pb_s_kernel(tc, h_ret, x, W1, b1, W2, b2, ln_g, ln_b, 
             )
         nc.sync.dma_start(out=bias_rows[0:4, :], in_=b1.rearrange("(r c) -> r c", c=2 * P))
         nc.sync.dma_start(out=bias_rows[4:6, :], in_=b2.rearrange("(r c) -> r c", c=2 * P))
-        nc.gpsimd.dma_start(out=x_sb[:], in_=x_rows)
         for i in range(PIECES):
             nc.sync.dma_start(out=w2_sb[:, i, :], in_=W2[P * i : P * (i + 1), :])
+        nc.sync.dma_start(out=x_sb[:], in_=x_rows)
         nc.sync.dma_start(out=norm_rows[0:2, :], in_=ln_g.rearrange("(r c) -> r c", c=2 * P))
         nc.sync.dma_start(out=norm_rows[2:4, :], in_=ln_b.rearrange("(r c) -> r c", c=2 * P))
         nc.scalar.activation(out=table_warm[:, 0:1], in_=table_warm[:, 0:1], func=ACT.Gelu)

@@ -32,11 +32,10 @@ def tile_simplifiedretnet_pb_s_kernel(tc, h_ret, x, W1, b1, W2, b2, ln_g, ln_b, 
         stage = stack.enter_context(tc.tile_pool(name="stage", bufs=4))
         psum_t = stack.enter_context(tc.psum_pool(name="psum_t", bufs=4))
         psum_z = stack.enter_context(tc.psum_pool(name="psum_z", bufs=2))
-        psum_o = stack.enter_context(tc.psum_pool(name="psum_o", bufs=2))
+        psum_v = stack.enter_context(tc.psum_pool(name="psum_v", bufs=1))
 
         ident = keep.tile([P, P], F32)
-        bias_rows = keep.tile([P, 2 * P], BF16)
-        norm_rows = keep.tile([P, 2 * P], BF16)
+        vec_rows = keep.tile([P, 2 * P], BF16)
         h_sb = keep.tile([P, H], BF16)
         x_sb = keep.tile([P, D], BF16)
         w1_sb = keep.tile([P, PIECES, 2 * H], BF16)
@@ -50,8 +49,7 @@ def tile_simplifiedretnet_pb_s_kernel(tc, h_ret, x, W1, b1, W2, b2, ln_g, ln_b, 
         g_codes = keep.tile([P, 2 * P], U32, align_bytes=64)
         g_scales = keep.tile([P, 2 * P], U8, align_bytes=64)
         b1_cols = keep.tile([P, 8], F32)
-        b2_cols = keep.tile([P, 2], F32)
-        norm_cols = keep.tile([P, 4], F32)
+        vec_cols = keep.tile([P, 6], F32)
         table_warm = keep.tile([P, 2], F32)
         zeros = keep.tile([P, 2 * P], F32)
         xb = keep.tile([P, D], F32)
@@ -85,8 +83,7 @@ def tile_simplifiedretnet_pb_s_kernel(tc, h_ret, x, W1, b1, W2, b2, ln_g, ln_b, 
         for bank in range(2):
             idle_bank = psum_z.tile([P, 2 * P], F32, tag="z")
             nc.tensor.matmul(idle_bank[:], lhsT=zeros[:, 0:P], rhs=zeros[:], start=True, stop=True)
-        nc.vector.memset(bias_rows[:], 0.0)
-        nc.vector.memset(norm_rows[:], 0.0)
+        nc.vector.memset(vec_rows[:], 0.0)
         nc.vector.memset(table_warm[:], 1.0)
         nc.vector.memset(ident[:], 0.0)
         make_identity(nc, ident[:], nomemset=True)
@@ -96,13 +93,13 @@ def tile_simplifiedretnet_pb_s_kernel(tc, h_ret, x, W1, b1, W2, b2, ln_g, ln_b, 
                 out=w1_sb[:, j, :],
                 in_=W1[2 * P * j : 2 * P * (j + 1), :].rearrange("(p e) k -> p (e k)", e=2),
             )
-        nc.sync.dma_start(out=bias_rows[0:4, :], in_=b1.rearrange("(r c) -> r c", c=2 * P))
-        nc.sync.dma_start(out=bias_rows[4:6, :], in_=b2.rearrange("(r c) -> r c", c=2 * P))
+        nc.sync.dma_start(out=vec_rows[0:4, :], in_=b1.rearrange("(r c) -> r c", c=2 * P))
+        nc.sync.dma_start(out=vec_rows[4:6, :], in_=b2.rearrange("(r c) -> r c", c=2 * P))
+        nc.sync.dma_start(out=vec_rows[6:8, :], in_=ln_g.rearrange("(r c) -> r c", c=2 * P))
+        nc.sync.dma_start(out=vec_rows[8:10, :], in_=ln_b.rearrange("(r c) -> r c", c=2 * P))
         for i in range(PIECES):
             nc.sync.dma_start(out=w2_sb[:, i, :], in_=W2[P * i : P * (i + 1), :])
         nc.sync.dma_start(out=x_sb[:], in_=x_rows)
-        nc.sync.dma_start(out=norm_rows[0:2, :], in_=ln_g.rearrange("(r c) -> r c", c=2 * P))
-        nc.sync.dma_start(out=norm_rows[2:4, :], in_=ln_b.rearrange("(r c) -> r c", c=2 * P))
         nc.scalar.activation(out=table_warm[:, 0:1], in_=table_warm[:, 0:1], func=ACT.Gelu)
 
         quantise_rows(h_sb[:], h_codes[:], h_scales[:])
@@ -112,12 +109,12 @@ def tile_simplifiedretnet_pb_s_kernel(tc, h_ret, x, W1, b1, W2, b2, ln_g, ln_b, 
             cols = slice(a * P, (a + 1) * P)
             quantise_rows(w1_sb[:, a // 2, (a % 2) * H : (a % 2 + 1) * H], w1_codes[:, cols], w1_scales[:, cols])
 
-        bias_bank = psum_t.tile([P, P], F32, tag="bank")
-        nc.tensor.transpose(bias_bank[:], bias_rows[:].bitcast(F32), ident[:])
-        nc.vector.tensor_copy(out=b1_cols[:], in_=bias_bank[:, 0:4].bitcast(BF16))
-        nc.vector.tensor_copy(out=b2_cols[:], in_=bias_bank[:, 4:6])
-        b2_bank = psum_o.tile([P, 2, P], F32, tag="acc")
-        spread_over_partitions(b2_bank, b2_cols)
+        vec_bank = psum_t.tile([P, P], F32, tag="bank")
+        nc.tensor.transpose(vec_bank[:], vec_rows[:].bitcast(F32), ident[:])
+        nc.vector.tensor_copy(out=b1_cols[:], in_=vec_bank[:, 0:4].bitcast(BF16))
+        nc.vector.tensor_copy(out=vec_cols[:], in_=vec_bank[:, 4:10])
+        b2_bank = psum_v.tile([P, 2, P], F32, tag="b2")
+        spread_over_partitions(b2_bank, vec_cols[:, 0:2])
 
         nc.vector.tensor_tensor(
             out=xb[:], in0=x_sb[:], in1=b2_bank[:].rearrange("i r q -> i (r q)").bitcast(BF16), op=ALU.add
@@ -179,8 +176,12 @@ def tile_simplifiedretnet_pb_s_kernel(tc, h_ret, x, W1, b1, W2, b2, ln_g, ln_b, 
             bias=1.0,
         )
 
+        gb_bank = psum_v.tile([P, 4, P], F32, tag="gb")
+        spread_over_partitions(gb_bank, vec_cols[:, 2:6])
+        gb = gb_bank[:].rearrange("i r q -> i (r q)").bitcast(BF16)
+
         for half in range(2):
-            o_bank = psum_o.tile([P, D // 2], F32, tag="acc")
+            o_bank = psum_z.tile([P, D // 2], F32, tag="z")
             for c in range(2):
                 first = half * D + c * 2 * P
                 nc.tensor.matmul_mx(
@@ -202,12 +203,6 @@ def tile_simplifiedretnet_pb_s_kernel(tc, h_ret, x, W1, b1, W2, b2, ln_g, ln_b, 
                 op1=ALU.add,
                 accum_out=sums[:, half : half + 1],
             )
-        norm_bank = psum_t.tile([P, P], F32, tag="bank")
-        nc.tensor.transpose(norm_bank[:], norm_rows[:].bitcast(F32), ident[:])
-        nc.vector.tensor_copy(out=norm_cols[:], in_=norm_bank[:, 0:4])
-        gb_bank = psum_t.tile([P, 4, P], F32, tag="bank")
-        spread_over_partitions(gb_bank, norm_cols)
-        gb = gb_bank[:].rearrange("i r q -> i (r q)").bitcast(BF16)
 
         nc.vector.tensor_scalar(
             out=minus_mean[:], in0=sums[:, 0:1], scalar1=sums[:, 1:2], scalar2=-1.0 / D, op0=ALU.add, op1=ALU.mult

@@ -44,10 +44,10 @@ def tile_simplifiedretnet_pb_s_kernel(tc, h_ret, x, W1, b1, W2, b2, ln_g, ln_b, 
         h_scales = keep.tile([P, P], U8, align_bytes=64)
         w1_codes = keep.tile([P, F], U32, align_bytes=64)
         w1_scales = keep.tile([P, F], U8, align_bytes=64)
-        w2_codes = keep.tile([P, 2 * D], U32, align_bytes=64)
-        w2_scales = keep.tile([P, 2 * D], U8, align_bytes=64)
-        g_codes = keep.tile([P, 2 * P], U32, align_bytes=64)
-        g_scales = keep.tile([P, 2 * P], U8, align_bytes=64)
+        w2_codes = keep.tile([P, PIECES, 2, P], U32, align_bytes=64)
+        w2_scales = keep.tile([P, PIECES, 2, P], U8, align_bytes=64)
+        g_codes = keep.tile([P, 2, P], U32, align_bytes=64)
+        g_scales = keep.tile([P, 2, P], U8, align_bytes=64)
         b1_cols = keep.tile([P, 8], F32)
         vec_cols = keep.tile([P, 6], F32)
         table_warm = keep.tile([P, 2], F32)
@@ -57,72 +57,46 @@ def tile_simplifiedretnet_pb_s_kernel(tc, h_ret, x, W1, b1, W2, b2, ln_g, ln_b, 
         centred = keep.tile([P, D], F32)
         result = keep.tile([P, D], F32)
         squares = keep.tile([P, D], F32)
-        sums = keep.tile([P, 2], F32)
+        sums = keep.tile([P, PIECES], F32)
+        minus_means = keep.tile([P, PIECES], F32)
         minus_mean = keep.tile([P, 1], F32)
         square_sum = keep.tile([P, 1], F32)
         rstd = keep.tile([P, 1], F32)
 
-        def quantise(values, codes, scales):
-            nc.vector.quantize_mx(out=codes.bitcast(FP8X4), scales=scales, in_=values)
-
-        def quantise_rows(rows, codes, scales):
+        def turn(rows):
             words = rows.bitcast(F32)
             bank = psum_t.tile([P, 2, P], F32, tag="bank")
             for u in range(2):
                 nc.tensor.transpose(bank[:, u, :], words[:, u * P : (u + 1) * P], ident[:])
+            return bank
+
+        def empty(bank, copy):
             grouped = stage.tile([P, P, 2], F32, tag="grouped", align_bytes=64)
-            nc.scalar.copy(out=grouped[:], in_=bank[:].rearrange("q u r -> q r u"))
-            quantise(grouped[:].rearrange("q r u -> q (r u)").bitcast(BF16), codes, scales)
-            return grouped
+            copy(out=grouped[:], in_=bank[:].rearrange("q u r -> q r u"))
+            return grouped[:].rearrange("q r u -> q (r u)").bitcast(BF16)
+
+        def quantise(values, codes, scales):
+            nc.vector.quantize_mx(out=codes.bitcast(FP8X4), scales=scales, in_=values)
 
         def spread_over_partitions(bank, cols):
             for r in range(cols.shape[1]):
                 nc.tensor.transpose(bank[:, r, :], cols[:, r : r + 1].to_broadcast([P, P]), ident[:])
 
-        nc.gpsimd.memset(zeros[:], 0.0)
-        for bank in range(2):
-            idle_bank = psum_z.tile([P, 2 * P], F32, tag="z")
-            nc.tensor.matmul(idle_bank[:], lhsT=zeros[:, 0:P], rhs=zeros[:], start=True, stop=True)
-        nc.vector.memset(vec_rows[:], 0.0)
-        nc.vector.memset(table_warm[:], 1.0)
-        nc.vector.memset(ident[:], 0.0)
-        make_identity(nc, ident[:], nomemset=True)
-        nc.sync.dma_start(out=h_sb[:], in_=h_rows)
-        for j in range(PIECES):
-            nc.sync.dma_start(
-                out=w1_sb[:, j, :],
-                in_=W1[2 * P * j : 2 * P * (j + 1), :].rearrange("(p e) k -> p (e k)", e=2),
-            )
-        nc.sync.dma_start(out=vec_rows[0:4, :], in_=b1.rearrange("(r c) -> r c", c=2 * P))
-        nc.sync.dma_start(out=vec_rows[4:6, :], in_=b2.rearrange("(r c) -> r c", c=2 * P))
-        nc.sync.dma_start(out=vec_rows[6:8, :], in_=ln_g.rearrange("(r c) -> r c", c=2 * P))
-        nc.sync.dma_start(out=vec_rows[8:10, :], in_=ln_b.rearrange("(r c) -> r c", c=2 * P))
-        for i in range(PIECES):
-            nc.sync.dma_start(out=w2_sb[:, i, :], in_=W2[P * i : P * (i + 1), :])
-        nc.sync.dma_start(out=x_sb[:], in_=x_rows)
-        nc.scalar.activation(out=table_warm[:, 0:1], in_=table_warm[:, 0:1], func=ACT.Gelu)
+        def w1_unit(a):
+            return w1_sb[:, a // 2, (a % 2) * H : (a % 2 + 1) * H]
 
-        quantise_rows(h_sb[:], h_codes[:], h_scales[:])
-
-
-        for a in range(F // P):
+        def quantise_w1(a, values):
             cols = slice(a * P, (a + 1) * P)
-            quantise_rows(w1_sb[:, a // 2, (a % 2) * H : (a % 2 + 1) * H], w1_codes[:, cols], w1_scales[:, cols])
+            quantise(values, w1_codes[:, cols], w1_scales[:, cols])
 
-        vec_bank = psum_t.tile([P, P], F32, tag="bank")
-        nc.tensor.transpose(vec_bank[:], vec_rows[:].bitcast(F32), ident[:])
-        nc.vector.tensor_copy(out=b1_cols[:], in_=vec_bank[:, 0:4].bitcast(BF16))
-        nc.vector.tensor_copy(out=vec_cols[:], in_=vec_bank[:, 4:10])
-        b2_bank = psum_v.tile([P, 2, P], F32, tag="b2")
-        spread_over_partitions(b2_bank, vec_cols[:, 0:2])
+        def w2_unit(n):
+            return w2_sb[:, n // 2, (n % 2) * H : (n % 2 + 1) * H]
 
-        nc.vector.tensor_tensor(
-            out=xb[:], in0=x_sb[:], in1=b2_bank[:].rearrange("i r q -> i (r q)").bitcast(BF16), op=ALU.add
-        )
+        def quantise_w2(n, values):
+            quantise(values, w2_codes[:, n // 2, n % 2, :], w2_scales[:, n // 2, n % 2, :])
 
-        def hidden_pass(c):
+        def first_product(c):
             z_bank = psum_z.tile([P, 4, P], F32, tag="z")
-            g_plain = stage.tile([P, 4, P], BF16, tag="g_plain")
             for t in range(4):
                 a = 4 * c + t
                 nc.tensor.matmul_mx(
@@ -134,10 +108,16 @@ def tile_simplifiedretnet_pb_s_kernel(tc, h_ret, x, W1, b1, W2, b2, ln_g, ln_b, 
                     start=True,
                     stop=True,
                 )
+            return z_bank
+
+        def gelu(c, z_bank):
+            g_plain = stage.tile([P, 4, P], BF16, tag="g_plain")
             for t in range(4):
-                a = 4 * c + t
                 nc.scalar.activation(
-                    out=g_plain[:, t, :], in_=z_bank[:, t, :], func=ACT.Gelu, bias=b1_cols[:, a : a + 1]
+                    out=g_plain[:, t, :],
+                    in_=z_bank[:, t, :],
+                    func=ACT.Gelu,
+                    bias=b1_cols[:, 4 * c + t : 4 * c + t + 1],
                 )
             return g_plain
 
@@ -147,65 +127,112 @@ def tile_simplifiedretnet_pb_s_kernel(tc, h_ret, x, W1, b1, W2, b2, ln_g, ln_b, 
             return g_grouped[:].rearrange("p r t -> p (r t)")
 
         def quantise_g(c, g_grouped):
-            quantise(g_grouped, g_codes[:, c * P : (c + 1) * P], g_scales[:, c * P : (c + 1) * P])
+            quantise(g_grouped, g_codes[:, c, :], g_scales[:, c, :])
 
-        def quantise_w2(i):
-            for c in range(2):
-                first = (i // 2) * D + c * 2 * P + (i % 2) * P
-                grouped = quantise_rows(
-                    w2_sb[:, i, c * H : (c + 1) * H], w2_codes[:, first : first + P], w2_scales[:, first : first + P]
-                )
-            return grouped
+        nc.gpsimd.memset(zeros[:], 0.0)
+        nc.vector.memset(ident[:], 0.0)
+        nc.vector.memset(vec_rows[:], 0.0)
+        nc.vector.memset(table_warm[:], 1.0)
+        make_identity(nc, ident[:], nomemset=True)
+        nc.sync.dma_start(out=h_sb[:], in_=h_rows)
+        for j in range(PIECES):
+            nc.sync.dma_start(
+                out=w1_sb[:, j, :],
+                in_=W1[2 * P * j : 2 * P * (j + 1), :].rearrange("(p e) k -> p (e k)", e=2),
+            )
+            if j == 2:
+                nc.sync.dma_start(out=vec_rows[0:4, :], in_=b1.rearrange("(r c) -> r c", c=2 * P))
+                nc.sync.dma_start(out=vec_rows[4:6, :], in_=b2.rearrange("(r c) -> r c", c=2 * P))
+                nc.sync.dma_start(out=vec_rows[6:8, :], in_=ln_g.rearrange("(r c) -> r c", c=2 * P))
+                nc.sync.dma_start(out=vec_rows[8:10, :], in_=ln_b.rearrange("(r c) -> r c", c=2 * P))
+        for i in range(PIECES):
+            nc.sync.dma_start(out=w2_sb[:, i, :], in_=W2[P * i : P * (i + 1), :])
+        nc.sync.dma_start(out=x_sb[:], in_=x_rows)
 
-        g_plain = hidden_pass(0)
+        stack.enter_context(
+            tc.manual_schedule(engines={mybir.EngineType.PE, mybir.EngineType.Activation, mybir.EngineType.DVE})
+        )
+        nc.scalar.activation(out=table_warm[:, 0:1], in_=table_warm[:, 0:1], func=ACT.Gelu)
+        for bank in range(2):
+            idle_bank = psum_z.tile([P, 2 * P], F32, tag="z")
+            nc.tensor.matmul(idle_bank[:], lhsT=zeros[:, 0:P], rhs=zeros[:], start=True, stop=True)
+
+        quantise(empty(turn(h_sb[:]), nc.scalar.copy), h_codes[:], h_scales[:])
+        for a in range(8):
+            quantise_w1(a, empty(turn(w1_unit(a)), nc.scalar.copy))
+            if a == 5:
+                vec_bank = psum_t.tile([P, P], F32, tag="bank")
+                nc.tensor.transpose(vec_bank[:], vec_rows[:].bitcast(F32), ident[:])
+                nc.vector.tensor_copy(out=b1_cols[:], in_=vec_bank[:, 0:4].bitcast(BF16))
+                nc.vector.tensor_copy(out=vec_cols[:], in_=vec_bank[:, 4:10])
+        b2_bank = psum_v.tile([P, 2, P], F32, tag="b2")
+        spread_over_partitions(b2_bank, vec_cols[:, 0:2])
+
+        g_plain = gelu(0, first_product(0))
+        banks = [turn(w2_unit(n)) for n in range(3)]
+        values = [empty(banks[0], nc.vector.tensor_copy), empty(banks[1], nc.vector.tensor_copy)]
+        values.append(empty(banks[2], nc.scalar.copy))
         g_grouped = regroup_g(g_plain)
+        quantise_w2(0, values[0])
+        quantise_w2(1, values[1])
         quantise_g(0, g_grouped)
-        for i in (0, 1):
-            quantise_w2(i)
-
-        g_plain = hidden_pass(1)
+        g_plain = gelu(1, first_product(1))
+        nc.vector.tensor_tensor(
+            out=xb[:], in0=x_sb[:], in1=b2_bank[:].rearrange("i r q -> i (r q)").bitcast(BF16), op=ALU.add
+        )
+        values.append(empty(turn(w2_unit(3)), nc.scalar.copy))
         g_grouped = regroup_g(g_plain)
+        quantise_w2(2, values[2])
+        quantise_w2(3, values[3])
         quantise_g(1, g_grouped)
-        for i in (2, 3):
-            grouped = quantise_w2(i)
+        for n in range(4, 8):
+            last_values = empty(turn(w2_unit(n)), nc.scalar.copy)
+            quantise_w2(n, last_values)
         nc.scalar.activation(
             out=table_warm[:, 1:2],
-            in_=grouped[:, P - 1, :].bitcast(BF16)[:, 3:4],
+            in_=last_values[:, 4 * P - 1 : 4 * P],
             func=ACT.Abs_reciprocal_sqrt,
             scale=0.0,
             bias=1.0,
         )
-
         gb_bank = psum_v.tile([P, 4, P], F32, tag="gb")
         spread_over_partitions(gb_bank, vec_cols[:, 2:6])
         gb = gb_bank[:].rearrange("i r q -> i (r q)").bitcast(BF16)
 
-        for half in range(2):
-            o_bank = psum_z.tile([P, D // 2], F32, tag="z")
+        o_banks = []
+        for i in range(PIECES):
+            o_bank = psum_t.tile([P, P], F32, tag="bank")
             for c in range(2):
-                first = half * D + c * 2 * P
                 nc.tensor.matmul_mx(
                     out=o_bank[:],
-                    lhsT=g_codes[:, c * P : (c + 1) * P].bitcast(FP8X4),
-                    lhsT_scale=g_scales[:, c * P : (c + 1) * P],
-                    rhs=w2_codes[:, first : first + 2 * P].bitcast(FP8X4),
-                    rhs_scale=w2_scales[:, first : first + 2 * P],
+                    lhsT=g_codes[:, c, :].bitcast(FP8X4),
+                    lhsT_scale=g_scales[:, c, :],
+                    rhs=w2_codes[:, i, c, :].bitcast(FP8X4),
+                    rhs_scale=w2_scales[:, i, c, :],
                     start=(c == 0),
                     stop=(c == 1),
                 )
-            cols = slice(half * (D // 2), (half + 1) * (D // 2))
+            o_banks.append(o_bank)
+        for i in range(PIECES):
+            cols = slice(i * P, (i + 1) * P)
             nc.vector.scalar_tensor_tensor(
                 out=y[:, cols],
-                in0=o_bank[:],
+                in0=o_banks[i][:],
                 scalar=1.0,
                 in1=xb[:, cols],
                 op0=ALU.mult,
                 op1=ALU.add,
-                accum_out=sums[:, half : half + 1],
+                accum_out=sums[:, i : i + 1],
             )
 
         nc.vector.tensor_scalar(
-            out=minus_mean[:], in0=sums[:, 0:1], scalar1=sums[:, 1:2], scalar2=-1.0 / D, op0=ALU.add, op1=ALU.mult
+            out=minus_means[:],
+            in0=sums[:],
+            scalar1=-1.0 / D,
+            scalar2=None,
+            op0=ALU.mult,
+            op1=ALU.add,
+            accum_out=minus_mean[:],
         )
         nc.scalar.activation(
             out=squares[:], in_=y[:], func=ACT.Square, bias=minus_mean[:, 0:1], accum_out=square_sum[:]

@@ -146,8 +146,9 @@ def tile_simplifiedretnet_pb_s_kernel(tc, h_ret, x, W1, b1, W2, b2, ln_g, ln_b, 
                 nc.sync.dma_start(out=vec_rows[6:8, :], in_=ln_g.rearrange("(r c) -> r c", c=2 * P))
                 nc.sync.dma_start(out=vec_rows[8:10, :], in_=ln_b.rearrange("(r c) -> r c", c=2 * P))
         for i in range(PIECES):
+            if i == PIECES - 1:
+                nc.sync.dma_start(out=x_sb[:], in_=x_rows)
             nc.sync.dma_start(out=w2_sb[:, i, :], in_=W2[P * i : P * (i + 1), :])
-        nc.sync.dma_start(out=x_sb[:], in_=x_rows)
 
         stack.enter_context(
             tc.manual_schedule(engines={mybir.EngineType.PE, mybir.EngineType.Activation, mybir.EngineType.DVE})
@@ -158,20 +159,28 @@ def tile_simplifiedretnet_pb_s_kernel(tc, h_ret, x, W1, b1, W2, b2, ln_g, ln_b, 
             nc.tensor.matmul(idle_bank[:], lhsT=zeros[:, 0:P], rhs=zeros[:], start=True, stop=True)
 
         quantise(empty(turn(h_sb[:]), nc.scalar.copy), h_codes[:], h_scales[:])
-        for a in range(8):
+        for a in range(5):
             quantise_w1(a, empty(turn(w1_unit(a)), nc.scalar.copy))
-            if a == 5:
-                vec_bank = psum_t.tile([P, P], F32, tag="bank")
-                nc.tensor.transpose(vec_bank[:], vec_rows[:].bitcast(F32), ident[:])
-                nc.vector.tensor_copy(out=b1_cols[:], in_=vec_bank[:, 0:4].bitcast(BF16))
-                nc.vector.tensor_copy(out=vec_cols[:], in_=vec_bank[:, 4:10])
-        b2_bank = psum_v.tile([P, 2, P], F32, tag="b2")
-        spread_over_partitions(b2_bank, vec_cols[:, 0:2])
+        values_5 = empty(turn(w1_unit(5)), nc.scalar.copy)
+        values_6 = empty(turn(w1_unit(6)), nc.scalar.copy)
+        vec_bank = psum_v.tile([P, P], F32, tag="gb")
+        nc.tensor.transpose(vec_bank[:], vec_rows[:].bitcast(F32), ident[:])
+        nc.vector.tensor_copy(out=b1_cols[:], in_=vec_bank[:, 0:4].bitcast(BF16))
+        nc.vector.tensor_copy(out=vec_cols[:], in_=vec_bank[:, 4:10])
+        quantise_w1(5, values_5)
+        values_7 = empty(turn(w1_unit(7)), nc.vector.tensor_copy)
+        quantise_w1(6, values_6)
+        quantise_w1(7, values_7)
 
         g_plain = gelu(0, first_product(0))
         banks = [turn(w2_unit(n)) for n in range(3)]
-        values = [empty(banks[0], nc.vector.tensor_copy), empty(banks[1], nc.vector.tensor_copy)]
-        values.append(empty(banks[2], nc.scalar.copy))
+        b2_bank = psum_v.tile([P, 2, P], F32, tag="b2")
+        spread_over_partitions(b2_bank, vec_cols[:, 0:2])
+        values = [
+            empty(banks[0], nc.scalar.copy),
+            empty(banks[1], nc.vector.tensor_copy),
+            empty(banks[2], nc.scalar.copy),
+        ]
         g_grouped = regroup_g(g_plain)
         quantise_w2(0, values[0])
         quantise_w2(1, values[1])

@@ -35,7 +35,8 @@ def tile_simplifiedretnet_pb_s_kernel(tc, h_ret, x, W1, b1, W2, b2, ln_g, ln_b, 
         psum_v = stack.enter_context(tc.psum_pool(name="psum_v", bufs=1))
 
         ident = keep.tile([P, P], F32)
-        vec_rows = keep.tile([P, 2 * P], BF16)
+        bias_rows = keep.tile([P, 2 * P], BF16)
+        norm_rows = keep.tile([P, 2 * P], BF16)
         h_sb = keep.tile([P, H], BF16)
         x_sb = keep.tile([P, D], BF16)
         w1_sb = keep.tile([P, PIECES, 2 * H], BF16)
@@ -49,7 +50,8 @@ def tile_simplifiedretnet_pb_s_kernel(tc, h_ret, x, W1, b1, W2, b2, ln_g, ln_b, 
         g_codes = keep.tile([P, 2, P], U32, align_bytes=64)
         g_scales = keep.tile([P, 2, P], U8, align_bytes=64)
         b1_cols = keep.tile([P, 8], F32)
-        vec_cols = keep.tile([P, 6], F32)
+        b2_cols = keep.tile([P, 2], F32)
+        norm_cols = keep.tile([P, 4], F32)
         table_warm = keep.tile([P, 2], F32)
         zeros = keep.tile([P, 2 * P], F32)
         xb = keep.tile([P, D], F32)
@@ -131,7 +133,8 @@ def tile_simplifiedretnet_pb_s_kernel(tc, h_ret, x, W1, b1, W2, b2, ln_g, ln_b, 
 
         nc.gpsimd.memset(zeros[:], 0.0)
         nc.vector.memset(ident[:], 0.0)
-        nc.vector.memset(vec_rows[:], 0.0)
+        nc.vector.memset(bias_rows[:], 0.0)
+        nc.vector.memset(norm_rows[:], 0.0)
         nc.vector.memset(table_warm[:], 1.0)
         make_identity(nc, ident[:], nomemset=True)
         nc.sync.dma_start(out=h_sb[:], in_=h_rows)
@@ -141,14 +144,13 @@ def tile_simplifiedretnet_pb_s_kernel(tc, h_ret, x, W1, b1, W2, b2, ln_g, ln_b, 
                 in_=W1[2 * P * j : 2 * P * (j + 1), :].rearrange("(p e) k -> p (e k)", e=2),
             )
             if j == 2:
-                nc.sync.dma_start(out=vec_rows[0:4, :], in_=b1.rearrange("(r c) -> r c", c=2 * P))
-                nc.sync.dma_start(out=vec_rows[4:6, :], in_=b2.rearrange("(r c) -> r c", c=2 * P))
-                nc.sync.dma_start(out=vec_rows[6:8, :], in_=ln_g.rearrange("(r c) -> r c", c=2 * P))
-                nc.sync.dma_start(out=vec_rows[8:10, :], in_=ln_b.rearrange("(r c) -> r c", c=2 * P))
+                nc.sync.dma_start(out=bias_rows[0:4, :], in_=b1.rearrange("(r c) -> r c", c=2 * P))
+                nc.sync.dma_start(out=bias_rows[4:6, :], in_=b2.rearrange("(r c) -> r c", c=2 * P))
         for i in range(PIECES):
-            if i == PIECES - 1:
-                nc.sync.dma_start(out=x_sb[:], in_=x_rows)
             nc.sync.dma_start(out=w2_sb[:, i, :], in_=W2[P * i : P * (i + 1), :])
+        nc.sync.dma_start(out=x_sb[:], in_=x_rows)
+        nc.sync.dma_start(out=norm_rows[0:2, :], in_=ln_g.rearrange("(r c) -> r c", c=2 * P))
+        nc.sync.dma_start(out=norm_rows[2:4, :], in_=ln_b.rearrange("(r c) -> r c", c=2 * P))
 
         stack.enter_context(
             tc.manual_schedule(engines={mybir.EngineType.PE, mybir.EngineType.Activation, mybir.EngineType.DVE})
@@ -163,10 +165,10 @@ def tile_simplifiedretnet_pb_s_kernel(tc, h_ret, x, W1, b1, W2, b2, ln_g, ln_b, 
             quantise_w1(a, empty(turn(w1_unit(a)), nc.scalar.copy))
         values_5 = empty(turn(w1_unit(5)), nc.scalar.copy)
         values_6 = empty(turn(w1_unit(6)), nc.scalar.copy)
-        vec_bank = psum_v.tile([P, P], F32, tag="gb")
-        nc.tensor.transpose(vec_bank[:], vec_rows[:].bitcast(F32), ident[:])
-        nc.vector.tensor_copy(out=b1_cols[:], in_=vec_bank[:, 0:4].bitcast(BF16))
-        nc.vector.tensor_copy(out=vec_cols[:], in_=vec_bank[:, 4:10])
+        bias_bank = psum_v.tile([P, P], F32, tag="gb")
+        nc.tensor.transpose(bias_bank[:], bias_rows[:].bitcast(F32), ident[:])
+        nc.vector.tensor_copy(out=b1_cols[:], in_=bias_bank[:, 0:4].bitcast(BF16))
+        nc.vector.tensor_copy(out=b2_cols[:], in_=bias_bank[:, 4:6])
         quantise_w1(5, values_5)
         values_7 = empty(turn(w1_unit(7)), nc.vector.tensor_copy)
         quantise_w1(6, values_6)
@@ -175,7 +177,7 @@ def tile_simplifiedretnet_pb_s_kernel(tc, h_ret, x, W1, b1, W2, b2, ln_g, ln_b, 
         g_plain = gelu(0, first_product(0))
         banks = [turn(w2_unit(n)) for n in range(3)]
         b2_bank = psum_v.tile([P, 2, P], F32, tag="b2")
-        spread_over_partitions(b2_bank, vec_cols[:, 0:2])
+        spread_over_partitions(b2_bank, b2_cols)
         values = [
             empty(banks[0], nc.scalar.copy),
             empty(banks[1], nc.vector.tensor_copy),
@@ -186,14 +188,14 @@ def tile_simplifiedretnet_pb_s_kernel(tc, h_ret, x, W1, b1, W2, b2, ln_g, ln_b, 
         quantise_w2(1, values[1])
         quantise_g(0, g_grouped)
         g_plain = gelu(1, first_product(1))
-        nc.vector.tensor_tensor(
-            out=xb[:], in0=x_sb[:], in1=b2_bank[:].rearrange("i r q -> i (r q)").bitcast(BF16), op=ALU.add
-        )
         values.append(empty(turn(w2_unit(3)), nc.scalar.copy))
         g_grouped = regroup_g(g_plain)
         quantise_w2(2, values[2])
         quantise_w2(3, values[3])
         quantise_g(1, g_grouped)
+        nc.vector.tensor_tensor(
+            out=xb[:], in0=x_sb[:], in1=b2_bank[:].rearrange("i r q -> i (r q)").bitcast(BF16), op=ALU.add
+        )
         for n in range(4, 8):
             last_values = empty(turn(w2_unit(n)), nc.scalar.copy)
             quantise_w2(n, last_values)
@@ -204,9 +206,9 @@ def tile_simplifiedretnet_pb_s_kernel(tc, h_ret, x, W1, b1, W2, b2, ln_g, ln_b, 
             scale=0.0,
             bias=1.0,
         )
-        gb_bank = psum_v.tile([P, 4, P], F32, tag="gb")
-        spread_over_partitions(gb_bank, vec_cols[:, 2:6])
-        gb = gb_bank[:].rearrange("i r q -> i (r q)").bitcast(BF16)
+        norm_bank = psum_v.tile([P, P], F32, tag="gb")
+        nc.tensor.transpose(norm_bank[:], norm_rows[:].bitcast(F32), ident[:])
+        nc.vector.tensor_copy(out=norm_cols[:], in_=norm_bank[:, 0:4])
 
         o_banks = []
         for i in range(PIECES):
@@ -222,6 +224,9 @@ def tile_simplifiedretnet_pb_s_kernel(tc, h_ret, x, W1, b1, W2, b2, ln_g, ln_b, 
                     stop=(c == 1),
                 )
             o_banks.append(o_bank)
+        gb_bank = psum_v.tile([P, 4, P], F32, tag="gb")
+        spread_over_partitions(gb_bank, norm_cols)
+        gb = gb_bank[:].rearrange("i r q -> i (r q)").bitcast(BF16)
         for i in range(PIECES):
             cols = slice(i * P, (i + 1) * P)
             nc.vector.scalar_tensor_tensor(

@@ -29,7 +29,7 @@ def tile_simplifiedretnet_pb_s_kernel(tc, h_ret, x, W1, b1, W2, b2, ln_g, ln_b, 
 
     with ExitStack() as stack:
         keep = stack.enter_context(tc.tile_pool(name="keep", bufs=1))
-        stage = stack.enter_context(tc.tile_pool(name="stage", bufs=4))
+        stage = stack.enter_context(tc.tile_pool(name="stage", bufs=6))
         psum_t = stack.enter_context(tc.psum_pool(name="psum_t", bufs=4))
         psum_z = stack.enter_context(tc.psum_pool(name="psum_z", bufs=2))
         psum_v = stack.enter_context(tc.psum_pool(name="psum_v", bufs=1))
@@ -83,6 +83,9 @@ def tile_simplifiedretnet_pb_s_kernel(tc, h_ret, x, W1, b1, W2, b2, ln_g, ln_b, 
         def spread_over_partitions(bank, cols):
             for r in range(cols.shape[1]):
                 nc.tensor.transpose(bank[:, r, :], cols[:, r : r + 1].to_broadcast([P, P]), ident[:])
+
+        def idle_product(bank, columns):
+            nc.tensor.matmul(bank, lhsT=zeros[:, 0:P], rhs=zeros[:, 0:columns], start=True, stop=True)
 
         def w1_unit(a):
             return w1_sb[:, a // 2, (a % 2) * H : (a % 2 + 1) * H]
@@ -147,10 +150,11 @@ def tile_simplifiedretnet_pb_s_kernel(tc, h_ret, x, W1, b1, W2, b2, ln_g, ln_b, 
                 nc.sync.dma_start(out=bias_rows[0:4, :], in_=b1.rearrange("(r c) -> r c", c=2 * P))
                 nc.sync.dma_start(out=bias_rows[4:6, :], in_=b2.rearrange("(r c) -> r c", c=2 * P))
         for i in range(PIECES):
+            if i == PIECES - 1:
+                nc.sync.dma_start(out=x_sb[:], in_=x_rows)
+                nc.sync.dma_start(out=norm_rows[0:2, :], in_=ln_g.rearrange("(r c) -> r c", c=2 * P))
+                nc.sync.dma_start(out=norm_rows[2:4, :], in_=ln_b.rearrange("(r c) -> r c", c=2 * P))
             nc.sync.dma_start(out=w2_sb[:, i, :], in_=W2[P * i : P * (i + 1), :])
-        nc.sync.dma_start(out=x_sb[:], in_=x_rows)
-        nc.sync.dma_start(out=norm_rows[0:2, :], in_=ln_g.rearrange("(r c) -> r c", c=2 * P))
-        nc.sync.dma_start(out=norm_rows[2:4, :], in_=ln_b.rearrange("(r c) -> r c", c=2 * P))
 
         stack.enter_context(
             tc.manual_schedule(engines={mybir.EngineType.PE, mybir.EngineType.Activation, mybir.EngineType.DVE})
@@ -158,26 +162,28 @@ def tile_simplifiedretnet_pb_s_kernel(tc, h_ret, x, W1, b1, W2, b2, ln_g, ln_b, 
         nc.scalar.activation(out=table_warm[:, 0:1], in_=table_warm[:, 0:1], func=ACT.Gelu)
         for bank in range(2):
             idle_bank = psum_z.tile([P, 2 * P], F32, tag="z")
-            nc.tensor.matmul(idle_bank[:], lhsT=zeros[:, 0:P], rhs=zeros[:], start=True, stop=True)
+            idle_product(idle_bank[:], 2 * P)
 
         quantise(empty(turn(h_sb[:]), nc.scalar.copy), h_codes[:], h_scales[:])
-        for a in range(5):
+        small_bank = psum_v.tile([P, P // 2], F32, tag="b2")
+        for a in range(4):
             quantise_w1(a, empty(turn(w1_unit(a)), nc.scalar.copy))
-        values_5 = empty(turn(w1_unit(5)), nc.scalar.copy)
-        values_6 = empty(turn(w1_unit(6)), nc.scalar.copy)
+            if a % 2 == 1:
+                idle_product(small_bank[:], P // 2)
+        values = [empty(turn(w1_unit(a)), nc.scalar.copy) for a in (4, 5)]
         bias_bank = psum_v.tile([P, P], F32, tag="gb")
         nc.tensor.transpose(bias_bank[:], bias_rows[:].bitcast(F32), ident[:])
         nc.vector.tensor_copy(out=b1_cols[:], in_=bias_bank[:, 0:4].bitcast(BF16))
         nc.vector.tensor_copy(out=b2_cols[:], in_=bias_bank[:, 4:6])
-        quantise_w1(5, values_5)
+        quantise_w1(4, values[0])
+        quantise_w1(5, values[1])
+        values_6 = empty(turn(w1_unit(6)), nc.scalar.copy)
         values_7 = empty(turn(w1_unit(7)), nc.vector.tensor_copy)
         quantise_w1(6, values_6)
         quantise_w1(7, values_7)
 
         g_plain = gelu(0, first_product(0))
         banks = [turn(w2_unit(n)) for n in range(3)]
-        b2_bank = psum_v.tile([P, 2, P], F32, tag="b2")
-        spread_over_partitions(b2_bank, b2_cols)
         values = [
             empty(banks[0], nc.scalar.copy),
             empty(banks[1], nc.vector.tensor_copy),
@@ -187,16 +193,23 @@ def tile_simplifiedretnet_pb_s_kernel(tc, h_ret, x, W1, b1, W2, b2, ln_g, ln_b, 
         quantise_w2(0, values[0])
         quantise_w2(1, values[1])
         quantise_g(0, g_grouped)
-        g_plain = gelu(1, first_product(1))
-        values.append(empty(turn(w2_unit(3)), nc.scalar.copy))
-        g_grouped = regroup_g(g_plain)
         quantise_w2(2, values[2])
-        quantise_w2(3, values[3])
+        g_plain = gelu(1, first_product(1))
+        values = [empty(turn(w2_unit(n)), nc.scalar.copy) for n in (3, 4, 5)]
+        norm_bank = psum_v.tile([P, P], F32, tag="gb")
+        nc.tensor.transpose(norm_bank[:], norm_rows[:].bitcast(F32), ident[:])
+        b2_bank = psum_v.tile([P, 2, P], F32, tag="b2")
+        spread_over_partitions(b2_bank, b2_cols)
+        g_grouped = regroup_g(g_plain)
+        quantise_w2(3, values[0])
         quantise_g(1, g_grouped)
+        quantise_w2(4, values[1])
+        quantise_w2(5, values[2])
+        nc.vector.tensor_copy(out=norm_cols[:], in_=norm_bank[:, 0:4])
         nc.vector.tensor_tensor(
             out=xb[:], in0=x_sb[:], in1=b2_bank[:].rearrange("i r q -> i (r q)").bitcast(BF16), op=ALU.add
         )
-        for n in range(4, 8):
+        for n in (6, 7):
             last_values = empty(turn(w2_unit(n)), nc.scalar.copy)
             quantise_w2(n, last_values)
         nc.scalar.activation(
@@ -206,10 +219,6 @@ def tile_simplifiedretnet_pb_s_kernel(tc, h_ret, x, W1, b1, W2, b2, ln_g, ln_b, 
             scale=0.0,
             bias=1.0,
         )
-        norm_bank = psum_v.tile([P, P], F32, tag="gb")
-        nc.tensor.transpose(norm_bank[:], norm_rows[:].bitcast(F32), ident[:])
-        nc.vector.tensor_copy(out=norm_cols[:], in_=norm_bank[:, 0:4])
-
         o_banks = []
         for i in range(PIECES):
             o_bank = psum_t.tile([P, P], F32, tag="bank")

@@ -131,6 +131,14 @@ def tile_simplifiedretnet_pb_s_kernel(tc, h_ret, x, W1, b1, W2, b2, ln_g, ln_b, 
             nc.vector.tensor_copy(out=g_grouped[:], in_=g_plain[:].rearrange("p t r -> p r t"))
             return g_grouped[:].rearrange("p r t -> p (r t)")
 
+        def add_x_b2(cols):
+            nc.vector.tensor_tensor(
+                out=xb[:, cols],
+                in0=x_sb[:, cols],
+                in1=b2_bank[:].rearrange("i r q -> i (r q)").bitcast(BF16)[:, cols],
+                op=ALU.add,
+            )
+
         def quantise_g(c, g_grouped):
             quantise(g_grouped, g_codes[:, c, :], g_scales[:, c, :])
 
@@ -206,9 +214,7 @@ def tile_simplifiedretnet_pb_s_kernel(tc, h_ret, x, W1, b1, W2, b2, ln_g, ln_b, 
         quantise_w2(4, values[1])
         quantise_w2(5, values[2])
         nc.vector.tensor_copy(out=norm_cols[:], in_=norm_bank[:, 0:4])
-        nc.vector.tensor_tensor(
-            out=xb[:], in0=x_sb[:], in1=b2_bank[:].rearrange("i r q -> i (r q)").bitcast(BF16), op=ALU.add
-        )
+        add_x_b2(slice(0, (PIECES - 1) * P))
         for n in (6, 7):
             last_values = empty(turn(w2_unit(n)), nc.scalar.copy)
             quantise_w2(n, last_values)
@@ -238,6 +244,8 @@ def tile_simplifiedretnet_pb_s_kernel(tc, h_ret, x, W1, b1, W2, b2, ln_g, ln_b, 
         gb = gb_bank[:].rearrange("i r q -> i (r q)").bitcast(BF16)
         for i in range(PIECES):
             cols = slice(i * P, (i + 1) * P)
+            if i == 2:
+                add_x_b2(slice((PIECES - 1) * P, D))
             nc.vector.scalar_tensor_tensor(
                 out=y[:, cols],
                 in0=o_banks[i][:],

from contextlib import ExitStack

import concourse.mybir as mybir
from concourse.masks import make_identity

F32 = mybir.dt.float32
BF16 = mybir.dt.bfloat16
U32 = mybir.dt.uint32
U8 = mybir.dt.uint8
FP8X4 = mybir.dt.float8_e4m3fn_x4
ACT = mybir.ActivationFunctionType
ALU = mybir.AluOpType

P = 128
H = 512
F = 1024
D = 512
LN_EPS = 1e-5
PIECES = 4

FLOPS = 2 * P * H * F + 2 * P * F * D


def tile_simplifiedretnet_pb_s_kernel(tc, h_ret, x, W1, b1, W2, b2, ln_g, ln_b, out):
    nc = tc.nc
    h_rows = h_ret.flatten_outer_dims()
    x_rows = x.flatten_outer_dims()
    out_rows = out.flatten_outer_dims()

    with ExitStack() as stack:
        keep = stack.enter_context(tc.tile_pool(name="keep", bufs=1))
        stage = stack.enter_context(tc.tile_pool(name="stage", bufs=6))
        psum_t = stack.enter_context(tc.psum_pool(name="psum_t", bufs=4))
        psum_z = stack.enter_context(tc.psum_pool(name="psum_z", bufs=2))
        psum_v = stack.enter_context(tc.psum_pool(name="psum_v", bufs=1))

        ident = keep.tile([P, P], F32)
        bias_rows = keep.tile([P, 2 * P], BF16)
        norm_rows = keep.tile([P, 2 * P], BF16)
        h_sb = keep.tile([P, H], BF16)
        x_sb = keep.tile([P, D], BF16)
        w1_sb = keep.tile([P, PIECES, 2 * H], BF16)
        w2_sb = keep.tile([P, PIECES, F], BF16)
        h_codes = keep.tile([P, P], U32, align_bytes=64)
        h_scales = keep.tile([P, P], U8, align_bytes=64)
        w1_codes = keep.tile([P, F], U32, align_bytes=64)
        w1_scales = keep.tile([P, F], U8, align_bytes=64)
        w2_codes = keep.tile([P, PIECES, 2, P], U32, align_bytes=64)
        w2_scales = keep.tile([P, PIECES, 2, P], U8, align_bytes=64)
        g_codes = keep.tile([P, 2, P], U32, align_bytes=64)
        g_scales = keep.tile([P, 2, P], U8, align_bytes=64)
        b1_cols = keep.tile([P, 8], F32)
        b2_cols = keep.tile([P, 2], F32)
        norm_cols = keep.tile([P, 4], F32)
        table_warm = keep.tile([P, 2], F32)
        zeros = keep.tile([P, 2 * P], F32)
        xb = keep.tile([P, D], F32)
        y = keep.tile([P, D], F32)
        centred = keep.tile([P, D], F32)
        result = keep.tile([P, D], F32)
        squares = keep.tile([P, D], F32)
        sums = keep.tile([P, PIECES], F32)
        minus_means = keep.tile([P, PIECES], F32)
        minus_mean = keep.tile([P, 1], F32)
        square_sum = keep.tile([P, 1], F32)
        rstd = keep.tile([P, 1], F32)

        def turn(rows):
            words = rows.bitcast(F32)
            bank = psum_t.tile([P, 2, P], F32, tag="bank")
            for u in range(2):
                nc.tensor.transpose(bank[:, u, :], words[:, u * P : (u + 1) * P], ident[:])
            return bank

        def empty(bank, copy):
            grouped = stage.tile([P, P, 2], F32, tag="grouped", align_bytes=64)
            copy(out=grouped[:], in_=bank[:].rearrange("q u r -> q r u"))
            return grouped[:].rearrange("q r u -> q (r u)").bitcast(BF16)

        def quantise(values, codes, scales):
            nc.vector.quantize_mx(out=codes.bitcast(FP8X4), scales=scales, in_=values)

        def spread_over_partitions(bank, cols):
            for r in range(cols.shape[1]):
                nc.tensor.transpose(bank[:, r, :], cols[:, r : r + 1].to_broadcast([P, P]), ident[:])

        def idle_product(bank, columns):
            nc.tensor.matmul(bank, lhsT=zeros[:, 0:P], rhs=zeros[:, 0:columns], start=True, stop=True)

        def w1_unit(a):
            return w1_sb[:, a // 2, (a % 2) * H : (a % 2 + 1) * H]

        def quantise_w1(a, values):
            cols = slice(a * P, (a + 1) * P)
            quantise(values, w1_codes[:, cols], w1_scales[:, cols])

        def w2_unit(n):
            return w2_sb[:, n // 2, (n % 2) * H : (n % 2 + 1) * H]

        def quantise_w2(n, values):
            quantise(values, w2_codes[:, n // 2, n % 2, :], w2_scales[:, n // 2, n % 2, :])

        def first_product(c):
            z_bank = psum_z.tile([P, 4, P], F32, tag="z")
            for t in range(4):
                a = 4 * c + t
                nc.tensor.matmul_mx(
                    out=z_bank[:, t, :],
                    lhsT=w1_codes[:, a * P : (a + 1) * P].bitcast(FP8X4),
                    lhsT_scale=w1_scales[:, a * P : (a + 1) * P],
                    rhs=h_codes[:].bitcast(FP8X4),
                    rhs_scale=h_scales[:],
                    start=True,
                    stop=True,
                )
            return z_bank

        def gelu(c, z_bank):
            g_plain = stage.tile([P, 4, P], BF16, tag="g_plain")
            for t in range(4):
                nc.scalar.activation(
                    out=g_plain[:, t, :],
                    in_=z_bank[:, t, :],
                    func=ACT.Gelu,
                    bias=b1_cols[:, 4 * c + t : 4 * c + t + 1],
                )
            return g_plain

        def regroup_g(g_plain):
            g_grouped = stage.tile([P, P, 4], BF16, tag="g_grouped", align_bytes=64)
            nc.vector.tensor_copy(out=g_grouped[:], in_=g_plain[:].rearrange("p t r -> p r t"))
            return g_grouped[:].rearrange("p r t -> p (r t)")

        def add_x_b2(cols):
            nc.vector.tensor_tensor(
                out=xb[:, cols],
                in0=x_sb[:, cols],
                in1=b2_bank[:].rearrange("i r q -> i (r q)").bitcast(BF16)[:, cols],
                op=ALU.add,
            )

        def quantise_g(c, g_grouped):
            quantise(g_grouped, g_codes[:, c, :], g_scales[:, c, :])

        nc.gpsimd.memset(zeros[:], 0.0)
        nc.vector.memset(ident[:], 0.0)
        nc.vector.memset(bias_rows[:], 0.0)
        nc.vector.memset(norm_rows[:], 0.0)
        nc.vector.memset(table_warm[:], 1.0)
        make_identity(nc, ident[:], nomemset=True)
        nc.sync.dma_start(out=h_sb[:], in_=h_rows)
        for j in range(PIECES):
            nc.sync.dma_start(
                out=w1_sb[:, j, :],
                in_=W1[2 * P * j : 2 * P * (j + 1), :].rearrange("(p e) k -> p (e k)", e=2),
            )
            if j == 2:
                nc.sync.dma_start(out=bias_rows[0:4, :], in_=b1.rearrange("(r c) -> r c", c=2 * P))
                nc.sync.dma_start(out=bias_rows[4:6, :], in_=b2.rearrange("(r c) -> r c", c=2 * P))
        for i in range(PIECES):
            if i == PIECES - 1:
                nc.sync.dma_start(out=x_sb[:], in_=x_rows)
                nc.sync.dma_start(out=norm_rows[0:2, :], in_=ln_g.rearrange("(r c) -> r c", c=2 * P))
                nc.sync.dma_start(out=norm_rows[2:4, :], in_=ln_b.rearrange("(r c) -> r c", c=2 * P))
            nc.sync.dma_start(out=w2_sb[:, i, :], in_=W2[P * i : P * (i + 1), :])

        stack.enter_context(
            tc.manual_schedule(engines={mybir.EngineType.PE, mybir.EngineType.Activation, mybir.EngineType.DVE})
        )
        nc.scalar.activation(out=table_warm[:, 0:1], in_=table_warm[:, 0:1], func=ACT.Gelu)
        for bank in range(2):
            idle_bank = psum_z.tile([P, 2 * P], F32, tag="z")
            idle_product(idle_bank[:], 2 * P)

        quantise(empty(turn(h_sb[:]), nc.scalar.copy), h_codes[:], h_scales[:])
        small_bank = psum_v.tile([P, P // 2], F32, tag="b2")
        for a in range(4):
            quantise_w1(a, empty(turn(w1_unit(a)), nc.scalar.copy))
            if a % 2 == 1:
                idle_product(small_bank[:], P // 2)
        values = [empty(turn(w1_unit(a)), nc.scalar.copy) for a in (4, 5)]
        bias_bank = psum_v.tile([P, P], F32, tag="gb")
        nc.tensor.transpose(bias_bank[:], bias_rows[:].bitcast(F32), ident[:])
        nc.vector.tensor_copy(out=b1_cols[:], in_=bias_bank[:, 0:4].bitcast(BF16))
        nc.vector.tensor_copy(out=b2_cols[:], in_=bias_bank[:, 4:6])
        quantise_w1(4, values[0])
        quantise_w1(5, values[1])
        values_6 = empty(turn(w1_unit(6)), nc.scalar.copy)
        values_7 = empty(turn(w1_unit(7)), nc.vector.tensor_copy)
        quantise_w1(6, values_6)
        quantise_w1(7, values_7)

        g_plain = gelu(0, first_product(0))
        banks = [turn(w2_unit(n)) for n in range(3)]
        values = [
            empty(banks[0], nc.scalar.copy),
            empty(banks[1], nc.vector.tensor_copy),
            empty(banks[2], nc.scalar.copy),
        ]
        g_grouped = regroup_g(g_plain)
        quantise_w2(0, values[0])
        quantise_w2(1, values[1])
        quantise_g(0, g_grouped)
        quantise_w2(2, values[2])
        g_plain = gelu(1, first_product(1))
        values = [empty(turn(w2_unit(n)), nc.scalar.copy) for n in (3, 4, 5)]
        norm_bank = psum_v.tile([P, P], F32, tag="gb")
        nc.tensor.transpose(norm_bank[:], norm_rows[:].bitcast(F32), ident[:])
        b2_bank = psum_v.tile([P, 2, P], F32, tag="b2")
        spread_over_partitions(b2_bank, b2_cols)
        g_grouped = regroup_g(g_plain)
        quantise_w2(3, values[0])
        quantise_g(1, g_grouped)
        quantise_w2(4, values[1])
        quantise_w2(5, values[2])
        nc.vector.tensor_copy(out=norm_cols[:], in_=norm_bank[:, 0:4])
        add_x_b2(slice(0, (PIECES - 1) * P))
        for n in (6, 7):
            last_values = empty(turn(w2_unit(n)), nc.scalar.copy)
            quantise_w2(n, last_values)
        nc.scalar.activation(
            out=table_warm[:, 1:2],
            in_=last_values[:, 4 * P - 1 : 4 * P],
            func=ACT.Abs_reciprocal_sqrt,
            scale=0.0,
            bias=1.0,
        )
        o_banks = []
        for i in range(PIECES):
            o_bank = psum_t.tile([P, P], F32, tag="bank")
            for c in range(2):
                nc.tensor.matmul_mx(
                    out=o_bank[:],
                    lhsT=g_codes[:, c, :].bitcast(FP8X4),
                    lhsT_scale=g_scales[:, c, :],
                    rhs=w2_codes[:, i, c, :].bitcast(FP8X4),
                    rhs_scale=w2_scales[:, i, c, :],
                    start=(c == 0),
                    stop=(c == 1),
                )
            o_banks.append(o_bank)
        gb_bank = psum_v.tile([P, 4, P], F32, tag="gb")
        spread_over_partitions(gb_bank, norm_cols)
        gb = gb_bank[:].rearrange("i r q -> i (r q)").bitcast(BF16)
        for i in range(PIECES):
            cols = slice(i * P, (i + 1) * P)
            if i == 2:
                add_x_b2(slice((PIECES - 1) * P, D))
            nc.vector.scalar_tensor_tensor(
                out=y[:, cols],
                in0=o_banks[i][:],
                scalar=1.0,
                in1=xb[:, cols],
                op0=ALU.mult,
                op1=ALU.add,
                accum_out=sums[:, i : i + 1],
            )

        nc.vector.tensor_scalar(
            out=minus_means[:],
            in0=sums[:],
            scalar1=-1.0 / D,
            scalar2=None,
            op0=ALU.mult,
            op1=ALU.add,
            accum_out=minus_mean[:],
        )
        nc.scalar.activation(
            out=squares[:], in_=y[:], func=ACT.Square, bias=minus_mean[:, 0:1], accum_out=square_sum[:]
        )
        nc.vector.scalar_tensor_tensor(
            out=centred[:], in0=y[:], scalar=minus_mean[:, 0:1], in1=gb[:, 0:D], op0=ALU.add, op1=ALU.mult
        )
        nc.scalar.activation(
            out=rstd[:], in_=square_sum[:], func=ACT.Abs_reciprocal_sqrt, bias=LN_EPS, scale=1.0 / D
        )
        for half in range(2):
            cols = slice(half * (D // 2), (half + 1) * (D // 2))
            nc.vector.scalar_tensor_tensor(
                out=result[:, cols],
                in0=centred[:, cols],
                scalar=rstd[:, 0:1],
                in1=gb[:, D + half * (D // 2) : D + (half + 1) * (D // 2)],
                op0=ALU.mult,
                op1=ALU.add,
            )
            nc.sync.dma_start(out=out_rows[:, cols], in_=result[:, cols])
